import numpy as np
import ml_dtypes


def mxq(x, axis, fmt="e4m3"):
    dtype, down = {"e4m3": (ml_dtypes.float8_e4m3fn, 7), "e5m2": (ml_dtypes.float8_e5m2, 14)}[fmt]
    v = np.moveaxis(np.asarray(x, np.float32).astype(ml_dtypes.bfloat16).astype(np.float64), axis, -1)
    blocks = v.reshape(v.shape[:-1] + (-1, 32))
    amax = np.abs(blocks).max(-1, keepdims=True)
    byte = np.maximum(np.where(amax > 0, np.frexp(amax)[1] - 1 + 127, 0) - down, 1)
    scale = np.exp2(byte - 127.0)
    codes = (blocks / scale).astype(np.float32).astype(dtype).astype(np.float64)
    return np.moveaxis((codes * scale).reshape(v.shape), -1, axis)


WIDE = False


def mx_kscale(k):
    if not WIDE:
        return np.ones(k)
    levels = np.array([10, -10, 5, -5, 0])
    a = np.random.permutation(np.resize(levels, k // 512 * 4)).reshape(k // 512, 4)
    idx = np.arange(k)
    return np.exp2(a[idx // 512, idx % 128 // 32])


BF16 = ml_dtypes.bfloat16


def bf(x):
    return np.asarray(x, np.float32).astype(BF16)


def f64(x):
    return np.asarray(x).astype(np.float64)


E2M1 = np.array([0.0, 0.5, 1.0, 1.5, 2.0, 3.0, 4.0, 6.0, -0.0, -0.5, -1.0, -1.5, -2.0, -3.0, -4.0, -6.0])


def pack_weight(w, fmt):
    k, n = w.shape
    w = f64(bf(w)).reshape(k // 32, 32, n)
    amax = np.abs(w).max(1)
    if fmt == "e4m3":
        byte = np.frexp(amax)[1] - 1 + 127 - 7
    else:
        mant, ex = np.frexp(amax / 6.0)
        byte = np.where(mant > 0.5, ex, ex - 1) + 127
    byte = np.clip(np.where(amax > 0, byte, 1), 1, 254)
    scaled = (w * np.exp2(127.0 - byte)[:, None, :]).reshape(k, n).astype(np.float32)
    by_word = np.ascontiguousarray(scaled.reshape(k // 512, 128, 4, n).transpose(0, 1, 3, 2))
    if fmt == "e4m3":
        words = by_word.astype(ml_dtypes.float8_e4m3fn).view(np.uint8)
    else:
        c = by_word.astype(ml_dtypes.float4_e2m1fn).view(np.uint8) & 0xF
        words = c[..., 0::2] | (c[..., 1::2] << 4)
    return np.ascontiguousarray(words), np.ascontiguousarray(byte.astype(np.uint8).reshape(k // 512, 16, n))


def unpack_weight(words, scales, fmt):
    g, p, n, _ = words.shape
    if fmt == "e4m3":
        vals = np.ascontiguousarray(words).view(ml_dtypes.float8_e4m3fn).astype(np.float64)
    else:
        nib = np.empty((g, p, n, 4), np.uint8)
        nib[..., 0::2] = words & 0xF
        nib[..., 1::2] = words >> 4
        vals = E2M1[nib]
    vals = vals * np.repeat(np.exp2(scales.astype(np.float64) - 127.0), 8, axis=1)[..., None]
    return vals.transpose(0, 1, 3, 2).reshape(g * 512, n)

def pack4(w):
    words, scales = pack_weight(w, "e2m1")
    return words.reshape(words.shape[0], 128, -1), scales


def unpack4(words, scales):
    return unpack_weight(words.reshape(words.shape[0], 128, -1, 2), scales, "e2m1")


B, G, DB, DR = 512, 16, 512, 1024


def mish(v):
    return v * np.tanh(np.log(1.0 + np.exp(v)))


def setup_inputs():
    s, t = mx_kscale(DR), mx_kscale(DB)
    BB_feature = bf(np.random.standard_normal((B, G, DB)) * t)
    RF_feature = bf(np.random.standard_normal((B, DR)) * s)
    W_bbbb = np.random.standard_normal((DB, DB)) / np.sqrt(DB) / t
    b_bbbb = bf(np.random.standard_normal(DB) * 0.5)
    W_rfbb = np.random.standard_normal((DB, DR)) / np.sqrt(DR) / s
    b_rfbb = bf(np.random.standard_normal(DB) * 0.5)
    W_bbbb_words, W_bbbb_scales = pack4(np.ascontiguousarray(W_bbbb.T))
    W_rfbb_words, W_rfbb_scales = pack4(np.ascontiguousarray(W_rfbb.T))
    return {"BB_feature": BB_feature,
            "RF_feature": RF_feature,
            "W_bbbb_words": W_bbbb_words,
            "W_bbbb_scales": W_bbbb_scales,
            "b_bbbb": b_bbbb,
            "W_rfbb_words": W_rfbb_words,
            "W_rfbb_scales": W_rfbb_scales,
            "b_rfbb": b_rfbb}


def reference(BB_feature, RF_feature, W_bbbb_words, W_bbbb_scales, b_bbbb, W_rfbb_words, W_rfbb_scales, b_rfbb):
    RF_to_BB = mish((mxq(f64(RF_feature), 1, "e4m3") @ unpack4(W_rfbb_words, W_rfbb_scales)) + f64(b_rfbb))
    BB_to_BB = mish((mxq(f64(BB_feature), 2, "e4m3") @ unpack4(W_bbbb_words, W_bbbb_scales)) + f64(b_bbbb))
    return BB_to_BB + RF_to_BB[:, None, :]

@@ -1,0 +1,232 @@
+from contextlib import ExitStack
+
+import concourse.mybir as mybir
+from concourse.masks import make_identity
+
+F32 = mybir.dt.float32
+BF16 = mybir.dt.bfloat16
+I32 = mybir.dt.int32
+U32 = mybir.dt.uint32
+U8 = mybir.dt.uint8
+FP8X4 = mybir.dt.float8_e4m3fn_x4
+FP4X4 = mybir.dt.float4_e2m1fn_x4
+ACT = mybir.ActivationFunctionType
+ALU = mybir.AluOpType
+
+P = 128
+K_PASS = 4 * P
+WORDS = K_PASS // 2
+SAMPLES, GROUPS, D_BB, D_RF, D_OUT = 512, 16, 512, 1024, 512
+SAMPLE_BLOCKS = SAMPLES // P
+BLOCKS = 4
+COLS = BLOCKS * P
+N_BLOCKS = D_OUT // P
+QUARTERS = GROUPS // BLOCKS
+RF_PASSES = D_RF // K_PASS
+UNITS = 1 + SAMPLE_BLOCKS * QUARTERS
+ROUNDS = RF_PASSES + SAMPLE_BLOCKS * QUARTERS
+W_PASSES = RF_PASSES + 1
+FEATURE_BUFS = 6
+LN_FLOOR = 2.0**-40
+
+FLOPS = 2 * SAMPLES * GROUPS * D_BB * D_OUT + 2 * SAMPLES * D_RF * D_OUT
+
+
+def tile_gnn_layer_pb_t_kernel(
+    tc, BB_feature, RF_feature, W_bbbb_words, W_bbbb_scales, b_bbbb, W_rfbb_words, W_rfbb_scales, b_rfbb, out
+):
+    nc = tc.nc
+    batches = [list(range(1 + QUARTERS * c, 1 + QUARTERS * (c + 1))) for c in range(SAMPLE_BLOCKS)]
+    batches[0] = [0] + batches[0]
+
+    with ExitStack() as stack:
+        keep = stack.enter_context(tc.tile_pool(name="keep", bufs=1))
+        ring = stack.enter_context(tc.tile_pool(name="ring", bufs=2))
+        psum = stack.enter_context(tc.psum_pool(name="psum", bufs=2))
+        stack.enter_context(tc.manual_schedule())
+
+        features = {}
+
+        def load_features(r):
+            if r >= ROUNDS:
+                return
+            if r < RF_PASSES:
+                piece = RF_feature.rearrange("(c s) k -> s c k", s=P)[:, :, r * K_PASS : (r + 1) * K_PASS]
+            else:
+                c, j = divmod(r - RF_PASSES, QUARTERS)
+                piece = BB_feature[c * P : (c + 1) * P, j * BLOCKS : (j + 1) * BLOCKS, :]
+            features[r] = ring.tile([P, BLOCKS, K_PASS], BF16, name="features", tag="features", bufs=FEATURE_BUFS)
+            nc.sync.dma_start(out=features[r][:], in_=piece)
+
+        bias_rows = keep.tile([P, P], BF16)
+        nc.vector.memset(bias_rows[:], 0.0)
+        nc.sync.dma_start(out=bias_rows[0:N_BLOCKS, :], in_=b_rfbb.rearrange("(r n) -> r n", n=P))
+        nc.sync.dma_start(out=bias_rows[N_BLOCKS : 2 * N_BLOCKS, :], in_=b_bbbb.rearrange("(r n) -> r n", n=P))
+
+        for r in range(RF_PASSES):
+            load_features(r)
+
+        w_words = keep.tile([P, W_PASSES, 2 * D_OUT], U8, align_bytes=64)
+        w_scales = keep.tile([P, W_PASSES, D_OUT], U8, align_bytes=64)
+        nc.vector.memset(w_scales[:].bitcast(I32), 0)
+        nc.sync.dma_start(
+            out=w_words[:, 0:RF_PASSES, :].bitcast(I32), in_=W_rfbb_words.bitcast(I32).rearrange("g p w -> p g w")
+        )
+        nc.sync.dma_start(out=w_words[:, RF_PASSES, :].bitcast(I32), in_=W_bbbb_words.bitcast(I32)[0])
+        for quadrant in range(4):
+            live = slice(32 * quadrant, 32 * quadrant + 4)
+            rows = slice(4 * quadrant, 4 * quadrant + 4)
+            nc.sync.dma_start(
+                out=w_scales[live, 0:RF_PASSES, :].bitcast(I32),
+                in_=W_rfbb_scales.bitcast(I32)[:, rows, :].rearrange("g r n -> r g n"),
+            )
+            nc.sync.dma_start(out=w_scales[live, RF_PASSES, :].bitcast(I32), in_=W_bbbb_scales.bitcast(I32)[0, rows, :])
+
+        for r in range(RF_PASSES, FEATURE_BUFS):
+            load_features(r)
+
+        identity = keep.tile([P, P], F32)
+        make_identity(nc, identity[:])
+        ln_floor = keep.tile([P, 1], F32)
+        nc.vector.memset(ln_floor[:], LN_FLOOR)
+
+        bias_square = keep.tile([P, P], F32)
+        nc.vector.tensor_copy(out=bias_square[:], in_=bias_rows[:])
+        bias_turned = psum.tile([P, COLS], F32, tag="turned")
+        nc.tensor.transpose(bias_turned[:, 0:P], bias_square[:], identity[:])
+        bias = keep.tile([P, 2 * N_BLOCKS], F32)
+        nc.vector.tensor_copy(out=bias[:], in_=bias_turned[:, 0 : 2 * N_BLOCKS])
+        minus_bias = keep.tile([P, 2 * N_BLOCKS], F32)
+        nc.vector.tensor_scalar_mul(out=minus_bias[:], in0=bias_turned[:, 0 : 2 * N_BLOCKS], scalar1=-1.0)
+
+        codes = keep.tile([P, ROUNDS, COLS], U32, align_bytes=64)
+        code_scales = keep.tile([P, ROUNDS, COLS], U8, align_bytes=64)
+
+        def quantise(r):
+            words = features[r][:].bitcast(F32)
+            grouped = ring.tile([P, BLOCKS, P, 2], F32, tag="grouped", bufs=3, align_bytes=64)
+            for half in range(2):
+                flipped = psum.tile([P, 2, 2, P], F32, tag="turned")
+                for i in range(2):
+                    for u in range(2):
+                        nc.tensor.transpose(flipped[:, i, u, :], words[:, 2 * half + i, u:WORDS:2], identity[:])
+                nc.vector.tensor_copy(
+                    out=grouped[:, 2 * half : 2 * half + 2, :, :], in_=flipped[:].rearrange("p i u s -> p i s u")
+                )
+            nc.vector.quantize_mx(
+                out=codes[:, r, :].bitcast(FP8X4),
+                scales=code_scales[:, r, :],
+                in_=grouped[:].rearrange("p i s u -> p (i s u)").bitcast(BF16),
+            )
+            load_features(r + FEATURE_BUFS)
+
+        def product(unit, nb, tag, bufs):
+            if unit == 0:
+                passes = [(g, g) for g in range(RF_PASSES)]
+            else:
+                passes = [(RF_PASSES, RF_PASSES + unit - 1)]
+            acc = psum.tile([P, COLS], F32, name="acc", tag=tag, bufs=bufs)
+            for g, (w, r) in enumerate(passes):
+                nc.tensor.matmul_mx(
+                    out=acc[:],
+                    lhsT=w_words[:, w, 2 * P * nb : 2 * P * (nb + 1)].bitcast(FP4X4),
+                    lhsT_scale=w_scales[:, w, P * nb : P * (nb + 1)],
+                    rhs=codes[:, r, :].bitcast(FP8X4),
+                    rhs_scale=code_scales[:, r, :],
+                    start=(g == 0),
+                    stop=(g == len(passes) - 1),
+                )
+            return acc
+
+        def bias_column(table, unit, nb):
+            column = nb if unit == 0 else N_BLOCKS + nb
+            return table[:, column : column + 1]
+
+        gates = {}
+        mished = {}
+
+        def sigmoid(unit):
+            gates[unit] = ring.tile([P, N_BLOCKS, COLS], F32, name="gate", tag="gate", bufs=len(batches[0]) + 3)
+            for nb in range(N_BLOCKS):
+                acc = product(unit, nb, "first", 4)
+                nc.scalar.activation(
+                    out=gates[unit][:, nb, :], in_=acc[:], func=ACT.Sigmoid, bias=bias_column(minus_bias, unit, nb), scale=-1.0
+                )
+
+        def log(unit):
+            nc.scalar.activation(out=gates[unit][:], in_=gates[unit][:], func=ACT.Ln, bias=ln_floor[:], scale=1.0)
+
+        def tanh(unit):
+            nc.scalar.activation(out=gates[unit][:], in_=gates[unit][:], func=ACT.Tanh, scale=-1.0)
+
+        def multiply(unit, half):
+            if half == 0:
+                mished[unit] = ring.tile([P, N_BLOCKS, COLS], F32, name="mish", tag="mish", bufs=3)
+            for nb in (2 * half, 2 * half + 1):
+                acc = product(unit, nb, "second", 2)
+                nc.vector.scalar_tensor_tensor(
+                    out=mished[unit][:, nb, :],
+                    in0=acc[:],
+                    scalar=bias_column(bias, unit, nb),
+                    in1=gates[unit][:, nb, :],
+                    op0=ALU.add,
+                    op1=ALU.mult,
+                )
+
+        rf_term = keep.tile([P, SAMPLE_BLOCKS, D_OUT], F32)
+
+        def turn(unit, half):
+            if unit > 0:
+                c, j = divmod(unit - 1, QUARTERS)
+                result = ring.tile([P, 2, D_OUT], F32, tag="result", bufs=4)
+            for i in range(2):
+                block = 2 * half + i
+                turned = psum.tile([P, D_OUT], F32, tag="turned")
+                for nb in range(N_BLOCKS):
+                    nc.tensor.transpose(
+                        turned[:, nb * P : (nb + 1) * P], mished[unit][:, nb, block * P : (block + 1) * P], identity[:]
+                    )
+                if unit == 0:
+                    nc.vector.tensor_copy(out=rf_term[:, block, :], in_=turned[:])
+                else:
+                    nc.vector.tensor_tensor(out=result[:, i, :], in0=turned[:], in1=rf_term[:, c, :], op=ALU.add)
+            if unit > 0:
+                first_group = j * BLOCKS + 2 * half
+                nc.sync.dma_start(out=out[c * P : (c + 1) * P, first_group : first_group + 2, :], in_=result[:])
+
+        def rounds_of(batch):
+            first = 0 if batch[0] == 0 else RF_PASSES + batch[0] - 1
+            return range(first, RF_PASSES + batch[-1])
+
+        def pick(units, s):
+            return units[s] if 0 <= s < len(units) else None
+
+        ahead = RF_PASSES + 1
+        for r in range(ahead):
+            quantise(r)
+        for unit in batches[0]:
+            sigmoid(unit)
+            quantise(unit + ahead)
+        for r in range(batches[0][-1] + ahead + 1, rounds_of(batches[2])[-1] + 1):
+            quantise(r)
+        for unit in batches[0]:
+            log(unit)
+
+        for b in range(1, len(batches) + 1):
+            entering = batches[b] if b < len(batches) else []
+            leaving = batches[b - 1]
+            for s in range(max(len(entering), len(leaving)) + 2):
+                if pick(entering, s) is not None:
+                    sigmoid(pick(entering, s))
+                for half in range(2):
+                    if pick(leaving, s - 1) is not None:
+                        multiply(pick(leaving, s - 1), half)
+                    if pick(leaving, s - 2) is not None:
+                        turn(pick(leaving, s - 2), half)
+                if pick(leaving, s) is not None:
+                    tanh(pick(leaving, s))
+            for unit in entering:
+                log(unit)
+            if b + 2 < len(batches):
+                for r in rounds_of(batches[b + 2]):
+                    quantise(r)

@@ -26,7 +26,8 @@ RF_PASSES = D_RF // K_PASS
 UNITS = 1 + SAMPLE_BLOCKS * QUARTERS
 ROUNDS = RF_PASSES + SAMPLE_BLOCKS * QUARTERS
 W_PASSES = RF_PASSES + 1
-FEATURE_BUFS = 6
+FEATURE_BUFS = 4
+FIRST_BATCH = 9
 LN_FLOOR = 2.0**-40
 
 FLOPS = 2 * SAMPLES * GROUPS * D_BB * D_OUT + 2 * SAMPLES * D_RF * D_OUT
@@ -36,8 +37,12 @@ def tile_gnn_layer_pb_t_kernel(
     tc, BB_feature, RF_feature, W_bbbb_words, W_bbbb_scales, b_bbbb, W_rfbb_words, W_rfbb_scales, b_rfbb, out
 ):
     nc = tc.nc
-    batches = [list(range(1 + QUARTERS * c, 1 + QUARTERS * (c + 1))) for c in range(SAMPLE_BLOCKS)]
-    batches[0] = [0] + batches[0]
+    batches = []
+    size = FIRST_BATCH
+    while sum(len(batch) for batch in batches) < UNITS:
+        start = sum(len(batch) for batch in batches)
+        batches.append(list(range(start, min(start + size, UNITS))))
+        size = (size + 1) // 2
 
     with ExitStack() as stack:
         keep = stack.enter_context(tc.tile_pool(name="keep", bufs=1))
@@ -104,7 +109,7 @@ def tile_gnn_layer_pb_t_kernel(
 
         def quantise(r):
             words = features[r][:].bitcast(F32)
-            grouped = ring.tile([P, BLOCKS, P, 2], F32, tag="grouped", bufs=3, align_bytes=64)
+            grouped = ring.tile([P, BLOCKS, P, 2], F32, tag="grouped", bufs=2, align_bytes=64)
             for half in range(2):
                 flipped = psum.tile([P, 2, 2, P], F32, tag="turned")
                 for i in range(2):
@@ -146,7 +151,7 @@ def tile_gnn_layer_pb_t_kernel(
         mished = {}
 
         def sigmoid(unit):
-            gates[unit] = ring.tile([P, N_BLOCKS, COLS], F32, name="gate", tag="gate", bufs=len(batches[0]) + 3)
+            gates[unit] = ring.tile([P, N_BLOCKS, COLS], F32, name="gate", tag="gate", bufs=FIRST_BATCH + 3)
             for nb in range(N_BLOCKS):
                 acc = product(unit, nb, "first", 4)
                 nc.scalar.activation(
@@ -157,7 +162,9 @@ def tile_gnn_layer_pb_t_kernel(
             nc.scalar.activation(out=gates[unit][:], in_=gates[unit][:], func=ACT.Ln, bias=ln_floor[:], scale=1.0)
 
         def tanh(unit):
-            nc.scalar.activation(out=gates[unit][:], in_=gates[unit][:], func=ACT.Tanh, scale=-1.0)
+            for half in range(2):
+                part = gates[unit][:, 2 * half : 2 * half + 2, :]
+                nc.scalar.activation(out=part, in_=part, func=ACT.Tanh, scale=-1.0)
 
         def multiply(unit, half):
             if half == 0:
@@ -178,7 +185,7 @@ def tile_gnn_layer_pb_t_kernel(
         def turn(unit, half):
             if unit > 0:
                 c, j = divmod(unit - 1, QUARTERS)
-                result = ring.tile([P, 2, D_OUT], F32, tag="result", bufs=4)
+                result = ring.tile([P, 2, D_OUT], F32, tag="result", bufs=3)
             for i in range(2):
                 block = 2 * half + i
                 turned = psum.tile([P, D_OUT], F32, tag="turned")
@@ -194,20 +201,15 @@ def tile_gnn_layer_pb_t_kernel(
                 first_group = j * BLOCKS + 2 * half
                 nc.sync.dma_start(out=out[c * P : (c + 1) * P, first_group : first_group + 2, :], in_=result[:])
 
-        def rounds_of(batch):
-            first = 0 if batch[0] == 0 else RF_PASSES + batch[0] - 1
-            return range(first, RF_PASSES + batch[-1])
-
         def pick(units, s):
             return units[s] if 0 <= s < len(units) else None
 
-        ahead = RF_PASSES + 1
-        for r in range(ahead):
+        for r in range(RF_PASSES + 1):
             quantise(r)
         for unit in batches[0]:
             sigmoid(unit)
-            quantise(unit + ahead)
-        for r in range(batches[0][-1] + ahead + 1, rounds_of(batches[2])[-1] + 1):
+            quantise(unit + RF_PASSES + 1)
+        for r in range(FIRST_BATCH + RF_PASSES + 1, ROUNDS):
             quantise(r)
         for unit in batches[0]:
             log(unit)
@@ -227,6 +229,3 @@ def tile_gnn_layer_pb_t_kernel(
                     tanh(pick(leaving, s))
             for unit in entering:
                 log(unit)
-            if b + 2 < len(batches):
-                for r in rounds_of(batches[b + 2]):
-                    quantise(r)

@@ -16,19 +16,30 @@ ALU = mybir.AluOpType
 P = 128
 K_PASS = 4 * P
 WORDS = K_PASS // 2
+WORDS_PER_CODE_WORD = 2
 SAMPLES, GROUPS, D_BB, D_RF, D_OUT = 512, 16, 512, 1024, 512
 SAMPLE_BLOCKS = SAMPLES // P
 BLOCKS = 4
 COLS = BLOCKS * P
 N_BLOCKS = D_OUT // P
 QUARTERS = GROUPS // BLOCKS
+RF_UNIT = 0
 RF_PASSES = D_RF // K_PASS
 UNITS = 1 + SAMPLE_BLOCKS * QUARTERS
 ROUNDS = RF_PASSES + SAMPLE_BLOCKS * QUARTERS
 W_PASSES = RF_PASSES + 1
-FEATURE_BUFS = 4
-FIRST_BATCH = 9
+QUADRANTS, QUADRANT = 4, 32
+SCALE_ROWS = QUADRANT // 8
 LN_FLOOR = 2.0**-40
+
+FIRST_BATCH = 9
+FIRST_BANKS = N_BLOCKS
+PAIR = 2
+FEATURE_BUFS = 4
+GROUPED_BUFS = 2
+GATE_BUFS = FIRST_BATCH + 3
+MISH_BUFS = 3
+RESULT_BUFS = 6
 
 FLOPS = 2 * SAMPLES * GROUPS * D_BB * D_OUT + 2 * SAMPLES * D_RF * D_OUT
 
@@ -46,8 +57,8 @@ def tile_gnn_layer_pb_t_kernel(
 
     with ExitStack() as stack:
         keep = stack.enter_context(tc.tile_pool(name="keep", bufs=1))
-        ring = stack.enter_context(tc.tile_pool(name="ring", bufs=2))
-        psum = stack.enter_context(tc.psum_pool(name="psum", bufs=2))
+        ring = stack.enter_context(tc.tile_pool(name="ring", bufs=1))
+        psum = stack.enter_context(tc.psum_pool(name="psum", bufs=PAIR))
         stack.enter_context(tc.manual_schedule())
 
         features = {}
@@ -63,13 +74,13 @@ def tile_gnn_layer_pb_t_kernel(
             features[r] = ring.tile([P, BLOCKS, K_PASS], BF16, name="features", tag="features", bufs=FEATURE_BUFS)
             nc.sync.dma_start(out=features[r][:], in_=piece)
 
+        for r in range(RF_PASSES):
+            load_features(r)
+
         bias_rows = keep.tile([P, P], BF16)
         nc.vector.memset(bias_rows[:], 0.0)
         nc.sync.dma_start(out=bias_rows[0:N_BLOCKS, :], in_=b_rfbb.rearrange("(r n) -> r n", n=P))
         nc.sync.dma_start(out=bias_rows[N_BLOCKS : 2 * N_BLOCKS, :], in_=b_bbbb.rearrange("(r n) -> r n", n=P))
-
-        for r in range(RF_PASSES):
-            load_features(r)
 
         w_words = keep.tile([P, W_PASSES, 2 * D_OUT], U8, align_bytes=64)
         w_scales = keep.tile([P, W_PASSES, D_OUT], U8, align_bytes=64)
@@ -78,9 +89,9 @@ def tile_gnn_layer_pb_t_kernel(
             out=w_words[:, 0:RF_PASSES, :].bitcast(I32), in_=W_rfbb_words.bitcast(I32).rearrange("g p w -> p g w")
         )
         nc.sync.dma_start(out=w_words[:, RF_PASSES, :].bitcast(I32), in_=W_bbbb_words.bitcast(I32)[0])
-        for quadrant in range(4):
-            live = slice(32 * quadrant, 32 * quadrant + 4)
-            rows = slice(4 * quadrant, 4 * quadrant + 4)
+        for quadrant in range(QUADRANTS):
+            live = slice(QUADRANT * quadrant, QUADRANT * quadrant + SCALE_ROWS)
+            rows = slice(SCALE_ROWS * quadrant, SCALE_ROWS * (quadrant + 1))
             nc.sync.dma_start(
                 out=w_scales[live, 0:RF_PASSES, :].bitcast(I32),
                 in_=W_rfbb_scales.bitcast(I32)[:, rows, :].rearrange("g r n -> r g n"),
@@ -92,31 +103,40 @@ def tile_gnn_layer_pb_t_kernel(
 
         identity = keep.tile([P, P], F32)
         make_identity(nc, identity[:])
+        identity_bf16 = keep.tile([P, P], BF16)
+        make_identity(nc, identity_bf16[:])
         ln_floor = keep.tile([P, 1], F32)
         nc.vector.memset(ln_floor[:], LN_FLOOR)
-
-        bias_square = keep.tile([P, P], F32)
-        nc.vector.tensor_copy(out=bias_square[:], in_=bias_rows[:])
-        bias_turned = psum.tile([P, COLS], F32, tag="turned")
-        nc.tensor.transpose(bias_turned[:, 0:P], bias_square[:], identity[:])
         bias = keep.tile([P, 2 * N_BLOCKS], F32)
-        nc.vector.tensor_copy(out=bias[:], in_=bias_turned[:, 0 : 2 * N_BLOCKS])
         minus_bias = keep.tile([P, 2 * N_BLOCKS], F32)
-        nc.vector.tensor_scalar_mul(out=minus_bias[:], in0=bias_turned[:, 0 : 2 * N_BLOCKS], scalar1=-1.0)
+
+        def turn_biases():
+            bias_turned = psum.tile([P, P], BF16, tag="turned")
+            nc.tensor.transpose(bias_turned[:], bias_rows[:], identity_bf16[:])
+            nc.vector.tensor_copy(out=bias[:], in_=bias_turned[:, 0 : 2 * N_BLOCKS])
+            nc.vector.tensor_scalar_mul(out=minus_bias[:], in0=bias_turned[:, 0 : 2 * N_BLOCKS], scalar1=-1.0)
+
+        def bias_column(table, unit, nb):
+            column = nb if unit == RF_UNIT else N_BLOCKS + nb
+            return table[:, column : column + 1]
 
         codes = keep.tile([P, ROUNDS, COLS], U32, align_bytes=64)
         code_scales = keep.tile([P, ROUNDS, COLS], U8, align_bytes=64)
 
         def quantise(r):
             words = features[r][:].bitcast(F32)
-            grouped = ring.tile([P, BLOCKS, P, 2], F32, tag="grouped", bufs=2, align_bytes=64)
-            for half in range(2):
-                flipped = psum.tile([P, 2, 2, P], F32, tag="turned")
-                for i in range(2):
-                    for u in range(2):
-                        nc.tensor.transpose(flipped[:, i, u, :], words[:, 2 * half + i, u:WORDS:2], identity[:])
+            grouped = ring.tile(
+                [P, BLOCKS, P, WORDS_PER_CODE_WORD], F32, name="grouped", tag="grouped", bufs=GROUPED_BUFS, align_bytes=64
+            )
+            for first in range(0, BLOCKS, PAIR):
+                flipped = psum.tile([P, PAIR, WORDS_PER_CODE_WORD, P], F32, tag="turned")
+                for i in range(PAIR):
+                    for u in range(WORDS_PER_CODE_WORD):
+                        nc.tensor.transpose(
+                            flipped[:, i, u, :], words[:, first + i, u:WORDS:WORDS_PER_CODE_WORD], identity[:]
+                        )
                 nc.vector.tensor_copy(
-                    out=grouped[:, 2 * half : 2 * half + 2, :, :], in_=flipped[:].rearrange("p i u s -> p i s u")
+                    out=grouped[:, first : first + PAIR, :, :], in_=flipped[:].rearrange("p i u s -> p i s u")
                 )
             nc.vector.quantize_mx(
                 out=codes[:, r, :].bitcast(FP8X4),
@@ -125,12 +145,12 @@ def tile_gnn_layer_pb_t_kernel(
             )
             load_features(r + FEATURE_BUFS)
 
-        def product(unit, nb, tag, bufs):
-            if unit == 0:
+        def product(unit, nb, tag, banks):
+            if unit == RF_UNIT:
                 passes = [(g, g) for g in range(RF_PASSES)]
             else:
                 passes = [(RF_PASSES, RF_PASSES + unit - 1)]
-            acc = psum.tile([P, COLS], F32, name="acc", tag=tag, bufs=bufs)
+            acc = psum.tile([P, COLS], F32, name="acc", tag=tag, bufs=banks)
             for g, (w, r) in enumerate(passes):
                 nc.tensor.matmul_mx(
                     out=acc[:],
@@ -143,34 +163,34 @@ def tile_gnn_layer_pb_t_kernel(
                 )
             return acc
 
-        def bias_column(table, unit, nb):
-            column = nb if unit == 0 else N_BLOCKS + nb
-            return table[:, column : column + 1]
-
         gates = {}
         mished = {}
 
         def sigmoid(unit):
-            gates[unit] = ring.tile([P, N_BLOCKS, COLS], F32, name="gate", tag="gate", bufs=FIRST_BATCH + 3)
+            gates[unit] = ring.tile([P, N_BLOCKS, COLS], F32, name="gate", tag="gate", bufs=GATE_BUFS)
             for nb in range(N_BLOCKS):
-                acc = product(unit, nb, "first", 4)
+                acc = product(unit, nb, "first", FIRST_BANKS)
                 nc.scalar.activation(
-                    out=gates[unit][:, nb, :], in_=acc[:], func=ACT.Sigmoid, bias=bias_column(minus_bias, unit, nb), scale=-1.0
+                    out=gates[unit][:, nb, :],
+                    in_=acc[:],
+                    func=ACT.Sigmoid,
+                    bias=bias_column(minus_bias, unit, nb),
+                    scale=-1.0,
                 )
 
         def log(unit):
             nc.scalar.activation(out=gates[unit][:], in_=gates[unit][:], func=ACT.Ln, bias=ln_floor[:], scale=1.0)
 
         def tanh(unit):
-            for half in range(2):
-                part = gates[unit][:, 2 * half : 2 * half + 2, :]
+            for first in range(0, N_BLOCKS, PAIR):
+                part = gates[unit][:, first : first + PAIR, :]
                 nc.scalar.activation(out=part, in_=part, func=ACT.Tanh, scale=-1.0)
 
-        def multiply(unit, half):
-            if half == 0:
-                mished[unit] = ring.tile([P, N_BLOCKS, COLS], F32, name="mish", tag="mish", bufs=3)
-            for nb in (2 * half, 2 * half + 1):
-                acc = product(unit, nb, "second", 2)
+        def multiply(unit, first):
+            if first == 0:
+                mished[unit] = ring.tile([P, N_BLOCKS, COLS], F32, name="mish", tag="mish", bufs=MISH_BUFS)
+            for nb in range(first, first + PAIR):
+                acc = product(unit, nb, "second", PAIR)
                 nc.vector.scalar_tensor_tensor(
                     out=mished[unit][:, nb, :],
                     in0=acc[:],
@@ -182,30 +202,25 @@ def tile_gnn_layer_pb_t_kernel(
 
         rf_term = keep.tile([P, SAMPLE_BLOCKS, D_OUT], F32)
 
-        def turn(unit, half):
-            if unit > 0:
-                c, j = divmod(unit - 1, QUARTERS)
-                result = ring.tile([P, 2, D_OUT], F32, tag="result", bufs=3)
-            for i in range(2):
-                block = 2 * half + i
+        def turn(unit, first):
+            for block in range(first, first + PAIR):
                 turned = psum.tile([P, D_OUT], F32, tag="turned")
                 for nb in range(N_BLOCKS):
                     nc.tensor.transpose(
                         turned[:, nb * P : (nb + 1) * P], mished[unit][:, nb, block * P : (block + 1) * P], identity[:]
                     )
-                if unit == 0:
+                if unit == RF_UNIT:
                     nc.vector.tensor_copy(out=rf_term[:, block, :], in_=turned[:])
                 else:
-                    nc.vector.tensor_tensor(out=result[:, i, :], in0=turned[:], in1=rf_term[:, c, :], op=ALU.add)
-            if unit > 0:
-                first_group = j * BLOCKS + 2 * half
-                nc.sync.dma_start(out=out[c * P : (c + 1) * P, first_group : first_group + 2, :], in_=result[:])
+                    c, j = divmod(unit - 1, QUARTERS)
+                    result = ring.tile([P, D_OUT], F32, tag="result", bufs=RESULT_BUFS)
+                    nc.vector.tensor_tensor(out=result[:], in0=turned[:], in1=rf_term[:, c, :], op=ALU.add)
+                    nc.sync.dma_start(out=out[c * P : (c + 1) * P, j * BLOCKS + block, :], in_=result[:])
 
-        def pick(units, s):
-            return units[s] if 0 <= s < len(units) else None
-
-        for r in range(RF_PASSES + 1):
+        for r in range(RF_PASSES):
             quantise(r)
+        turn_biases()
+        quantise(RF_PASSES)
         for unit in batches[0]:
             sigmoid(unit)
             quantise(unit + RF_PASSES + 1)
@@ -214,17 +229,20 @@ def tile_gnn_layer_pb_t_kernel(
         for unit in batches[0]:
             log(unit)
 
+        def pick(units, s):
+            return units[s] if 0 <= s < len(units) else None
+
         for b in range(1, len(batches) + 1):
             entering = batches[b] if b < len(batches) else []
             leaving = batches[b - 1]
             for s in range(max(len(entering), len(leaving)) + 2):
                 if pick(entering, s) is not None:
                     sigmoid(pick(entering, s))
-                for half in range(2):
+                for first in range(0, N_BLOCKS, PAIR):
                     if pick(leaving, s - 1) is not None:
-                        multiply(pick(leaving, s - 1), half)
+                        multiply(pick(leaving, s - 1), first)
                     if pick(leaving, s - 2) is not None:
-                        turn(pick(leaving, s - 2), half)
+                        turn(pick(leaving, s - 2), first)
                 if pick(leaving, s) is not None:
                     tanh(pick(leaving, s))
             for unit in entering:

@@ -32,13 +32,16 @@ QUADRANTS, QUADRANT = 4, 32
 SCALE_ROWS = QUADRANT // 8
 LN_FLOOR = 2.0**-40
 
-FIRST_BATCH = 9
+BATCH_SIZES = (9, 5, 3)
+SCALAR_BLOCKS = (1, 3)
+P1_LAG = 0
+LAY_SLOT = 0
+FIRST_BATCH = BATCH_SIZES[0]
 FIRST_BANKS = N_BLOCKS
 PAIR = 2
 FEATURE_BUFS = 4
 GROUPED_BUFS = 2
-GATE_BUFS = FIRST_BATCH + 3
-MISH_BUFS = 3
+GATE_BUFS = FIRST_BATCH + 4
 RESULT_BUFS = 6
 
 FLOPS = 2 * SAMPLES * GROUPS * D_BB * D_OUT + 2 * SAMPLES * D_RF * D_OUT
@@ -49,11 +52,9 @@ def tile_gnn_layer_pb_t_kernel(
 ):
     nc = tc.nc
     batches = []
-    size = FIRST_BATCH
-    while sum(len(batch) for batch in batches) < UNITS:
+    for size in BATCH_SIZES:
         start = sum(len(batch) for batch in batches)
-        batches.append(list(range(start, min(start + size, UNITS))))
-        size = (size + 1) // 2
+        batches.append(list(range(start, start + size)))
 
     with ExitStack() as stack:
         keep = stack.enter_context(tc.tile_pool(name="keep", bufs=1))
@@ -62,33 +63,50 @@ def tile_gnn_layer_pb_t_kernel(
         stack.enter_context(tc.manual_schedule())
 
         features = {}
+        entry_order = batches[0][1:] + [RF_UNIT]
+        round_order = []
+        rounds_needed = {}
+        for unit in entry_order:
+            round_order.extend(list(range(RF_PASSES)) if unit == RF_UNIT else [RF_PASSES + unit - 1])
+            rounds_needed[unit] = len(round_order)
+        round_order.extend(range(len(round_order), ROUNDS))
 
-        def load_features(r):
-            if r >= ROUNDS:
+        def load_features(position):
+            if position >= ROUNDS:
                 return
+            r = round_order[position]
             if r < RF_PASSES:
                 piece = RF_feature.rearrange("(c s) k -> s c k", s=P)[:, :, r * K_PASS : (r + 1) * K_PASS]
             else:
                 c, j = divmod(r - RF_PASSES, QUARTERS)
                 piece = BB_feature[c * P : (c + 1) * P, j * BLOCKS : (j + 1) * BLOCKS, :]
             features[r] = ring.tile([P, BLOCKS, K_PASS], BF16, name="features", tag="features", bufs=FEATURE_BUFS)
-            nc.sync.dma_start(out=features[r][:], in_=piece)
+            if position == 0:
+                for i in range(BLOCKS):
+                    nc.sync.dma_start(out=features[r][:, i, :], in_=piece[:, i, :])
+            else:
+                nc.sync.dma_start(out=features[r][:], in_=piece)
 
-        for r in range(RF_PASSES):
-            load_features(r)
+        load_features(0)
 
         bias_rows = keep.tile([P, P], BF16)
         nc.vector.memset(bias_rows[:], 0.0)
-        nc.sync.dma_start(out=bias_rows[0:N_BLOCKS, :], in_=b_rfbb.rearrange("(r n) -> r n", n=P))
-        nc.sync.dma_start(out=bias_rows[N_BLOCKS : 2 * N_BLOCKS, :], in_=b_bbbb.rearrange("(r n) -> r n", n=P))
+        nc.scalar.dma_start(out=bias_rows[0:N_BLOCKS, :], in_=b_rfbb.rearrange("(r n) -> r n", n=P))
+        nc.scalar.dma_start(out=bias_rows[N_BLOCKS : 2 * N_BLOCKS, :], in_=b_bbbb.rearrange("(r n) -> r n", n=P))
 
         w_words = keep.tile([P, W_PASSES, 2 * D_OUT], U8, align_bytes=64)
         w_scales = keep.tile([P, W_PASSES, D_OUT], U8, align_bytes=64)
         nc.vector.memset(w_scales[:].bitcast(I32), 0)
+        nc.sync.dma_start(out=w_words[:, RF_PASSES, :].bitcast(I32), in_=W_bbbb_words.bitcast(I32)[0])
+        for quadrant in range(QUADRANTS):
+            live = slice(QUADRANT * quadrant, QUADRANT * quadrant + SCALE_ROWS)
+            rows = slice(SCALE_ROWS * quadrant, SCALE_ROWS * (quadrant + 1))
+            nc.sync.dma_start(out=w_scales[live, RF_PASSES, :].bitcast(I32), in_=W_bbbb_scales.bitcast(I32)[0, rows, :])
+        for position in range(1, FEATURE_BUFS - 1):
+            load_features(position)
         nc.sync.dma_start(
             out=w_words[:, 0:RF_PASSES, :].bitcast(I32), in_=W_rfbb_words.bitcast(I32).rearrange("g p w -> p g w")
         )
-        nc.sync.dma_start(out=w_words[:, RF_PASSES, :].bitcast(I32), in_=W_bbbb_words.bitcast(I32)[0])
         for quadrant in range(QUADRANTS):
             live = slice(QUADRANT * quadrant, QUADRANT * quadrant + SCALE_ROWS)
             rows = slice(SCALE_ROWS * quadrant, SCALE_ROWS * (quadrant + 1))
@@ -96,10 +114,7 @@ def tile_gnn_layer_pb_t_kernel(
                 out=w_scales[live, 0:RF_PASSES, :].bitcast(I32),
                 in_=W_rfbb_scales.bitcast(I32)[:, rows, :].rearrange("g r n -> r g n"),
             )
-            nc.sync.dma_start(out=w_scales[live, RF_PASSES, :].bitcast(I32), in_=W_bbbb_scales.bitcast(I32)[0, rows, :])
-
-        for r in range(RF_PASSES, FEATURE_BUFS):
-            load_features(r)
+        load_features(FEATURE_BUFS - 1)
 
         identity = keep.tile([P, P], F32)
         make_identity(nc, identity[:])
@@ -123,7 +138,8 @@ def tile_gnn_layer_pb_t_kernel(
         codes = keep.tile([P, ROUNDS, COLS], U32, align_bytes=64)
         code_scales = keep.tile([P, ROUNDS, COLS], U8, align_bytes=64)
 
-        def quantise(r):
+        def quantise(position):
+            r = round_order[position]
             words = features[r][:].bitcast(F32)
             grouped = ring.tile(
                 [P, BLOCKS, P, WORDS_PER_CODE_WORD], F32, name="grouped", tag="grouped", bufs=GROUPED_BUFS, align_bytes=64
@@ -143,7 +159,7 @@ def tile_gnn_layer_pb_t_kernel(
                 scales=code_scales[:, r, :],
                 in_=grouped[:].rearrange("p i s u -> p (i s u)").bitcast(BF16),
             )
-            load_features(r + FEATURE_BUFS)
+            load_features(position + FEATURE_BUFS)
 
         def product(unit, nb, tag, banks):
             if unit == RF_UNIT:
@@ -163,16 +179,22 @@ def tile_gnn_layer_pb_t_kernel(
                 )
             return acc
 
+        rf_mish = keep.tile([P, N_BLOCKS, COLS], F32)
         gates = {}
         mished = {}
 
+        firsts = {}
+
+        def first_product(unit):
+            firsts[unit] = [product(unit, nb, "first", FIRST_BANKS) for nb in range(N_BLOCKS)]
+
         def sigmoid(unit):
-            gates[unit] = ring.tile([P, N_BLOCKS, COLS], F32, name="gate", tag="gate", bufs=GATE_BUFS)
+            if unit not in gates:
+                gates[unit] = ring.tile([P, N_BLOCKS, COLS], F32, name="gate", tag="gate", bufs=GATE_BUFS)
             for nb in range(N_BLOCKS):
-                acc = product(unit, nb, "first", FIRST_BANKS)
                 nc.scalar.activation(
                     out=gates[unit][:, nb, :],
-                    in_=acc[:],
+                    in_=firsts[unit][nb][:],
                     func=ACT.Sigmoid,
                     bias=bias_column(minus_bias, unit, nb),
                     scale=-1.0,
@@ -188,7 +210,7 @@ def tile_gnn_layer_pb_t_kernel(
 
         def multiply(unit, first):
             if first == 0:
-                mished[unit] = ring.tile([P, N_BLOCKS, COLS], F32, name="mish", tag="mish", bufs=MISH_BUFS)
+                mished[unit] = rf_mish if unit == RF_UNIT else gates[unit]
             for nb in range(first, first + PAIR):
                 acc = product(unit, nb, "second", PAIR)
                 nc.vector.scalar_tensor_tensor(
@@ -202,8 +224,41 @@ def tile_gnn_layer_pb_t_kernel(
 
         rf_term = keep.tile([P, SAMPLE_BLOCKS, D_OUT], F32)
 
-        def turn(unit, first):
+        def lay_rf(c):
+            bank = psum.tile([P, D_OUT], F32, name="acc", tag="first", bufs=FIRST_BANKS)
+            for nb in range(N_BLOCKS):
+                nc.tensor.matmul(
+                    bank[:, nb * P : (nb + 1) * P],
+                    lhsT=rf_mish[:, nb, c * P : (c + 1) * P],
+                    rhs=identity[:],
+                    is_transpose=True,
+                    start=(nb == 0),
+                    stop=False,
+                )
+            return bank
+
+        laid = {}
+
+        def turn(unit, first, shared=False):
             for block in range(first, first + PAIR):
+                if shared and block in SCALAR_BLOCKS:
+                    c, j = divmod(unit - 1, QUARTERS)
+                    bank = laid.get((unit, block))
+                    if bank is None:
+                        bank = lay_rf(c)
+                    for nb in range(N_BLOCKS):
+                        nc.tensor.matmul(
+                            bank[:, nb * P : (nb + 1) * P],
+                            lhsT=mished[unit][:, nb, block * P : (block + 1) * P],
+                            rhs=identity[:],
+                            is_transpose=True,
+                            start=False,
+                            stop=(nb == N_BLOCKS - 1),
+                        )
+                    result = ring.tile([P, D_OUT], F32, tag="result", bufs=RESULT_BUFS)
+                    nc.scalar.copy(out=result[:], in_=bank[:])
+                    nc.scalar.dma_start(out=out[c * P : (c + 1) * P, j * BLOCKS + block, :], in_=result[:])
+                    continue
                 turned = psum.tile([P, D_OUT], F32, tag="turned")
                 for nb in range(N_BLOCKS):
                     nc.tensor.transpose(
@@ -217,33 +272,62 @@ def tile_gnn_layer_pb_t_kernel(
                     nc.vector.tensor_tensor(out=result[:], in0=turned[:], in1=rf_term[:, c, :], op=ALU.add)
                     nc.sync.dma_start(out=out[c * P : (c + 1) * P, j * BLOCKS + block, :], in_=result[:])
 
-        for r in range(RF_PASSES):
-            quantise(r)
         turn_biases()
-        quantise(RF_PASSES)
-        for unit in batches[0]:
+        gates[RF_UNIT] = ring.tile([P, N_BLOCKS, COLS], F32, name="gate", tag="gate", bufs=GATE_BUFS)
+        quantised = 0
+        for unit in entry_order:
+            for position in range(quantised, rounds_needed[unit] + 1):
+                quantise(position)
+            quantised = rounds_needed[unit] + 1
+            first_product(unit)
             sigmoid(unit)
-            quantise(unit + RF_PASSES + 1)
-        for r in range(FIRST_BATCH + RF_PASSES + 1, ROUNDS):
-            quantise(r)
+        first_product(batches[1][0])
+        for position in range(quantised, ROUNDS):
+            quantise(position)
         for unit in batches[0]:
             log(unit)
 
         def pick(units, s):
             return units[s] if 0 <= s < len(units) else None
 
-        for b in range(1, len(batches) + 1):
-            entering = batches[b] if b < len(batches) else []
+        table_dummy = keep.tile([P, 1], F32)
+        nc.vector.memset(table_dummy[:], 0.0)
+
+        for b in range(1, len(batches)):
+            entering = batches[b]
             leaving = batches[b - 1]
-            for s in range(max(len(entering), len(leaving)) + 2):
-                if pick(entering, s) is not None:
-                    sigmoid(pick(entering, s))
+            upcoming = entering[1:] + (batches[b + 1][0:1] if b + 1 < len(batches) else [])
+            nc.scalar.activation(out=table_dummy[:], in_=table_dummy[:], func=ACT.Sigmoid)
+            for unit in leaving:
+                tanh(unit)
+            sigmoid(entering[0])
+            for s in range(len(leaving) + 1):
+                if b == len(batches) - 1 and s == len(leaving) + LAY_SLOT:
+                    for unit, block in [(unit, block) for unit in entering for block in SCALAR_BLOCKS][0:FIRST_BANKS]:
+                        laid[(unit, block)] = lay_rf((unit - 1) // QUARTERS)
                 for first in range(0, N_BLOCKS, PAIR):
+                    if pick(leaving, s) is not None:
+                        multiply(pick(leaving, s), first)
                     if pick(leaving, s - 1) is not None:
-                        multiply(pick(leaving, s - 1), first)
-                    if pick(leaving, s - 2) is not None:
-                        turn(pick(leaving, s - 2), first)
-                if pick(leaving, s) is not None:
-                    tanh(pick(leaving, s))
+                        turn(pick(leaving, s - 1), first)
+                    if s >= len(leaving) // 2 + P1_LAG and upcoming:
+                        first_product(upcoming[0])
+                        if upcoming[0] in entering:
+                            sigmoid(upcoming[0])
+                        upcoming = upcoming[1:]
+            for unit in upcoming:
+                first_product(unit)
+                if unit in entering:
+                    sigmoid(unit)
             for unit in entering:
                 log(unit)
+
+        leaving = batches[-1]
+        for unit in leaving:
+            tanh(unit)
+        for s in range(len(leaving) + 1):
+            for first in range(0, N_BLOCKS, PAIR):
+                if pick(leaving, s) is not None:
+                    multiply(pick(leaving, s), first)
+                if pick(leaving, s - 1) is not None:
+                    turn(pick(leaving, s - 1), first, shared=True)

@@ -32,10 +32,17 @@ QUADRANTS, QUADRANT = 4, 32
 SCALE_ROWS = QUADRANT // 8
 LN_FLOOR = 2.0**-40
 
-BATCH_SIZES = (9, 5, 3)
+GPSIMD_UNITS = 3
+BATCH_SIZES = (4, 4, 3, 3)
+ROOT = 128
+G_PHASE = (1, 2, 3)
+G_ORDER = "c0 c1 d0 c2 d1 d2"
+G_INVERT = ((0, 0), (1, 4), (2, 3))
 SCALAR_BLOCKS = (1, 3)
 P1_LAG = 0
-LAY_SLOT = 0
+FIRST_SPLIT = 1
+BIAS_RF_AT = 3
+LOG_LAG = 9
 FIRST_BATCH = BATCH_SIZES[0]
 FIRST_BANKS = N_BLOCKS
 PAIR = 2
@@ -63,13 +70,14 @@ def tile_gnn_layer_pb_t_kernel(
         stack.enter_context(tc.manual_schedule())
 
         features = {}
-        entry_order = batches[0][1:] + [RF_UNIT]
+        gpsimd_units = list(range(UNITS - GPSIMD_UNITS, UNITS))
+        entry_order = batches[0][1:] + [RF_UNIT] + gpsimd_units
         round_order = []
         rounds_needed = {}
         for unit in entry_order:
             round_order.extend(list(range(RF_PASSES)) if unit == RF_UNIT else [RF_PASSES + unit - 1])
             rounds_needed[unit] = len(round_order)
-        round_order.extend(range(len(round_order), ROUNDS))
+        round_order.extend([r for r in range(ROUNDS) if r not in round_order])
 
         def load_features(position):
             if position >= ROUNDS:
@@ -81,28 +89,30 @@ def tile_gnn_layer_pb_t_kernel(
                 c, j = divmod(r - RF_PASSES, QUARTERS)
                 piece = BB_feature[c * P : (c + 1) * P, j * BLOCKS : (j + 1) * BLOCKS, :]
             features[r] = ring.tile([P, BLOCKS, K_PASS], BF16, name="features", tag="features", bufs=FEATURE_BUFS)
-            if position == 0:
-                for i in range(BLOCKS):
-                    nc.sync.dma_start(out=features[r][:, i, :], in_=piece[:, i, :])
+            if position == 0 and FIRST_SPLIT > 1:
+                step = BLOCKS // FIRST_SPLIT
+                for i in range(0, BLOCKS, step):
+                    nc.sync.dma_start(out=features[r][:, i : i + step, :], in_=piece[:, i : i + step, :])
             else:
                 nc.sync.dma_start(out=features[r][:], in_=piece)
 
         load_features(0)
-
-        bias_rows = keep.tile([P, P], BF16)
-        nc.vector.memset(bias_rows[:], 0.0)
-        nc.scalar.dma_start(out=bias_rows[0:N_BLOCKS, :], in_=b_rfbb.rearrange("(r n) -> r n", n=P))
-        nc.scalar.dma_start(out=bias_rows[N_BLOCKS : 2 * N_BLOCKS, :], in_=b_bbbb.rearrange("(r n) -> r n", n=P))
+        load_features(1)
 
         w_words = keep.tile([P, W_PASSES, 2 * D_OUT], U8, align_bytes=64)
         w_scales = keep.tile([P, W_PASSES, D_OUT], U8, align_bytes=64)
         nc.vector.memset(w_scales[:].bitcast(I32), 0)
-        nc.sync.dma_start(out=w_words[:, RF_PASSES, :].bitcast(I32), in_=W_bbbb_words.bitcast(I32)[0])
+        bias_rows = {}
+        for kind in range(2):
+            bias_rows[kind] = keep.tile([P, P], BF16, name="bias_rows%d" % kind)
+            nc.vector.memset(bias_rows[kind][:], 0.0)
         for quadrant in range(QUADRANTS):
             live = slice(QUADRANT * quadrant, QUADRANT * quadrant + SCALE_ROWS)
             rows = slice(SCALE_ROWS * quadrant, SCALE_ROWS * (quadrant + 1))
             nc.sync.dma_start(out=w_scales[live, RF_PASSES, :].bitcast(I32), in_=W_bbbb_scales.bitcast(I32)[0, rows, :])
-        for position in range(1, FEATURE_BUFS - 1):
+        nc.sync.dma_start(out=w_words[:, RF_PASSES, :].bitcast(I32), in_=W_bbbb_words.bitcast(I32)[0])
+        nc.scalar.dma_start(out=bias_rows[1][0:N_BLOCKS, :], in_=b_bbbb.rearrange("(r n) -> r n", n=P))
+        for position in range(2, FEATURE_BUFS):
             load_features(position)
         nc.sync.dma_start(
             out=w_words[:, 0:RF_PASSES, :].bitcast(I32), in_=W_rfbb_words.bitcast(I32).rearrange("g p w -> p g w")
@@ -114,22 +124,25 @@ def tile_gnn_layer_pb_t_kernel(
                 out=w_scales[live, 0:RF_PASSES, :].bitcast(I32),
                 in_=W_rfbb_scales.bitcast(I32)[:, rows, :].rearrange("g r n -> r g n"),
             )
-        load_features(FEATURE_BUFS - 1)
+        nc.sync.dma_start(out=bias_rows[0][0:N_BLOCKS, :], in_=b_rfbb.rearrange("(r n) -> r n", n=P))
 
         identity = keep.tile([P, P], F32)
         make_identity(nc, identity[:])
         identity_bf16 = keep.tile([P, P], BF16)
         make_identity(nc, identity_bf16[:])
+        table_dummy = keep.tile([P, 1], F32)
+        nc.vector.memset(table_dummy[:], 0.0)
         ln_floor = keep.tile([P, 1], F32)
         nc.vector.memset(ln_floor[:], LN_FLOOR)
         bias = keep.tile([P, 2 * N_BLOCKS], F32)
         minus_bias = keep.tile([P, 2 * N_BLOCKS], F32)
 
-        def turn_biases():
+        def turn_bias(kind):
+            columns = slice(kind * N_BLOCKS, (kind + 1) * N_BLOCKS)
             bias_turned = psum.tile([P, P], BF16, tag="turned")
-            nc.tensor.transpose(bias_turned[:], bias_rows[:], identity_bf16[:])
-            nc.vector.tensor_copy(out=bias[:], in_=bias_turned[:, 0 : 2 * N_BLOCKS])
-            nc.vector.tensor_scalar_mul(out=minus_bias[:], in0=bias_turned[:, 0 : 2 * N_BLOCKS], scalar1=-1.0)
+            nc.tensor.transpose(bias_turned[:], bias_rows[kind][:], identity_bf16[:])
+            nc.vector.tensor_copy(out=bias[:, columns], in_=bias_turned[:, 0:N_BLOCKS])
+            nc.vector.tensor_scalar_mul(out=minus_bias[:, columns], in0=bias_turned[:, 0:N_BLOCKS], scalar1=-1.0)
 
         def bias_column(table, unit, nb):
             column = nb if unit == RF_UNIT else N_BLOCKS + nb
@@ -189,6 +202,8 @@ def tile_gnn_layer_pb_t_kernel(
             firsts[unit] = [product(unit, nb, "first", FIRST_BANKS) for nb in range(N_BLOCKS)]
 
         def sigmoid(unit):
+            if unit in gpsimd_units:
+                gates[unit] = ring.tile([P, N_BLOCKS, COLS], F32, name="gate_g", tag="gate_g", bufs=GPSIMD_UNITS)
             if unit not in gates:
                 gates[unit] = ring.tile([P, N_BLOCKS, COLS], F32, name="gate", tag="gate", bufs=GATE_BUFS)
             for nb in range(N_BLOCKS):
@@ -208,16 +223,55 @@ def tile_gnn_layer_pb_t_kernel(
                 part = gates[unit][:, first : first + PAIR, :]
                 nc.scalar.activation(out=part, in_=part, func=ACT.Tanh, scale=-1.0)
 
+        def slot(unit, nb):
+            return (nb + N_BLOCKS // 2) % N_BLOCKS if unit in gpsimd_units else nb
+
+        products = {}
+        roots = {}
+
+        def climb(unit):
+            leaves = gates[unit][:].rearrange("p a c -> p (a c)")
+            nc.gpsimd.tensor_tensor(out=leaves, in0=leaves, in1=leaves, op=ALU.mult)
+            nc.gpsimd.tensor_scalar(out=leaves, in0=leaves, scalar1=1.0, scalar2=1.0, op0=ALU.mult, op1=ALU.add)
+            products[unit] = [leaves]
+            width = N_BLOCKS * COLS // 2
+            while width >= ROOT:
+                node = ring.tile([P, width], F32, name="node%d" % width, tag="node%d" % width, bufs=PAIR)
+                below = products[unit][-1]
+                nc.gpsimd.tensor_tensor(out=node[:], in0=below[:, 0:width], in1=below[:, width : 2 * width], op=ALU.mult)
+                products[unit].append(node[:])
+                width = width // 2
+
+        def invert(unit):
+            root = ring.tile([P, ROOT], F32, name="root", tag="root", bufs=PAIR)
+            nc.vector.reciprocal(out=root[:], in_=products[unit][-1])
+            roots[unit] = root[:]
+
+        def descend(unit):
+            inverse = roots[unit]
+            width = ROOT
+            for level in reversed(products[unit][1:-1]):
+                lower = ring.tile([P, 2 * width], F32, name="lower%d" % width, tag="lower%d" % width, bufs=1)
+                nc.gpsimd.tensor_tensor(out=lower[:, 0:width], in0=level[:, width : 2 * width], in1=inverse, op=ALU.mult)
+                nc.gpsimd.tensor_tensor(out=lower[:, width : 2 * width], in0=level[:, 0:width], in1=inverse, op=ALU.mult)
+                inverse = lower[:]
+                width = 2 * width
+            leaves = products[unit][0]
+            for half in range(2):
+                part = leaves[:, half * width : (half + 1) * width]
+                nc.gpsimd.tensor_tensor(out=part, in0=part, in1=inverse, op=ALU.mult)
+            nc.gpsimd.tensor_scalar(out=leaves, in0=leaves, scalar1=2.0, scalar2=-1.0, op0=ALU.mult, op1=ALU.add)
+
         def multiply(unit, first):
             if first == 0:
                 mished[unit] = rf_mish if unit == RF_UNIT else gates[unit]
             for nb in range(first, first + PAIR):
                 acc = product(unit, nb, "second", PAIR)
                 nc.vector.scalar_tensor_tensor(
-                    out=mished[unit][:, nb, :],
+                    out=mished[unit][:, slot(unit, nb), :],
                     in0=acc[:],
                     scalar=bias_column(bias, unit, nb),
-                    in1=gates[unit][:, nb, :],
+                    in1=gates[unit][:, slot(unit, nb), :],
                     op0=ALU.add,
                     op1=ALU.mult,
                 )
@@ -249,7 +303,7 @@ def tile_gnn_layer_pb_t_kernel(
                     for nb in range(N_BLOCKS):
                         nc.tensor.matmul(
                             bank[:, nb * P : (nb + 1) * P],
-                            lhsT=mished[unit][:, nb, block * P : (block + 1) * P],
+                            lhsT=mished[unit][:, slot(unit, nb), block * P : (block + 1) * P],
                             rhs=identity[:],
                             is_transpose=True,
                             start=False,
@@ -262,7 +316,7 @@ def tile_gnn_layer_pb_t_kernel(
                 turned = psum.tile([P, D_OUT], F32, tag="turned")
                 for nb in range(N_BLOCKS):
                     nc.tensor.transpose(
-                        turned[:, nb * P : (nb + 1) * P], mished[unit][:, nb, block * P : (block + 1) * P], identity[:]
+                        turned[:, nb * P : (nb + 1) * P], mished[unit][:, slot(unit, nb), block * P : (block + 1) * P], identity[:]
                     )
                 if unit == RF_UNIT:
                     nc.vector.tensor_copy(out=rf_term[:, block, :], in_=turned[:])
@@ -272,62 +326,93 @@ def tile_gnn_layer_pb_t_kernel(
                     nc.vector.tensor_tensor(out=result[:], in0=turned[:], in1=rf_term[:, c, :], op=ALU.add)
                     nc.sync.dma_start(out=out[c * P : (c + 1) * P, j * BLOCKS + block, :], in_=result[:])
 
-        turn_biases()
         gates[RF_UNIT] = ring.tile([P, N_BLOCKS, COLS], F32, name="gate", tag="gate", bufs=GATE_BUFS)
         quantised = 0
         for unit in entry_order:
             for position in range(quantised, rounds_needed[unit] + 1):
                 quantise(position)
+                if position == 0:
+                    turn_bias(1)
+                if position == BIAS_RF_AT:
+                    turn_bias(0)
             quantised = rounds_needed[unit] + 1
             first_product(unit)
             sigmoid(unit)
-        first_product(batches[1][0])
         for position in range(quantised, ROUNDS):
             quantise(position)
         for unit in batches[0]:
             log(unit)
+        g_steps = G_ORDER.split()
+
+        def gpsimd_work(phase, s):
+            for i, unit in enumerate(gpsimd_units):
+                if G_INVERT[i] == (phase, s):
+                    while "c%d" % i in g_steps:
+                        step = g_steps[0]
+                        g_steps.remove(step)
+                        if step[0] == "c":
+                            climb(gpsimd_units[int(step[1:])])
+                        else:
+                            descend(gpsimd_units[int(step[1:])])
+                    invert(unit)
+            while g_steps and g_steps[0][0] == "d" and gpsimd_units[int(g_steps[0][1:])] in roots:
+                descend(gpsimd_units[int(g_steps[0][1:])])
+                g_steps.remove(g_steps[0])
+
+        gpsimd_work(0, 0)
 
         def pick(units, s):
             return units[s] if 0 <= s < len(units) else None
 
-        table_dummy = keep.tile([P, 1], F32)
-        nc.vector.memset(table_dummy[:], 0.0)
+        def slot_work(leaving, s, shared, between):
+            if shared and pick(leaving, s - 1) is not None:
+                for block in SCALAR_BLOCKS:
+                    laid[(pick(leaving, s - 1), block)] = lay_rf((pick(leaving, s - 1) - 1) // QUARTERS)
+            for first in range(0, N_BLOCKS, PAIR):
+                if pick(leaving, s) is not None:
+                    multiply(pick(leaving, s), first)
+                if pick(leaving, s - 1) is not None:
+                    turn(pick(leaving, s - 1), first, shared=shared)
+                between()
+
+        def nothing():
+            return None
 
         for b in range(1, len(batches)):
             entering = batches[b]
-            leaving = batches[b - 1]
-            upcoming = entering[1:] + (batches[b + 1][0:1] if b + 1 < len(batches) else [])
+            leaving = batches[b - 1] + [unit for i, unit in enumerate(gpsimd_units) if G_PHASE[i] == b]
+            upcoming = entering[1:]
+            logs = list(entering)
             nc.scalar.activation(out=table_dummy[:], in_=table_dummy[:], func=ACT.Sigmoid)
-            for unit in leaving:
+            for unit in batches[b - 1]:
                 tanh(unit)
+            first_product(entering[0])
             sigmoid(entering[0])
+
+            def next_sigmoid():
+                if upcoming:
+                    first_product(upcoming[0])
+                    sigmoid(upcoming[0])
+                    upcoming.remove(upcoming[0])
+
+            sigmoids_from = len(batches[b - 1]) // 2 + P1_LAG
+            logs_from = (len(batches[b - 1]) + len(entering)) // 2 + LOG_LAG
             for s in range(len(leaving) + 1):
-                if b == len(batches) - 1 and s == len(leaving) + LAY_SLOT:
-                    for unit, block in [(unit, block) for unit in entering for block in SCALAR_BLOCKS][0:FIRST_BANKS]:
-                        laid[(unit, block)] = lay_rf((unit - 1) // QUARTERS)
-                for first in range(0, N_BLOCKS, PAIR):
-                    if pick(leaving, s) is not None:
-                        multiply(pick(leaving, s), first)
-                    if pick(leaving, s - 1) is not None:
-                        turn(pick(leaving, s - 1), first)
-                    if s >= len(leaving) // 2 + P1_LAG and upcoming:
-                        first_product(upcoming[0])
-                        if upcoming[0] in entering:
-                            sigmoid(upcoming[0])
-                        upcoming = upcoming[1:]
-            for unit in upcoming:
-                first_product(unit)
-                if unit in entering:
-                    sigmoid(unit)
-            for unit in entering:
+                gpsimd_work(b, s)
+                if s >= logs_from:
+                    while upcoming:
+                        next_sigmoid()
+                    if logs:
+                        log(logs[0])
+                        logs.remove(logs[0])
+                slot_work(leaving, s, s >= logs_from, next_sigmoid if s >= sigmoids_from else nothing)
+            while upcoming:
+                next_sigmoid()
+            for unit in logs:
                 log(unit)
 
         leaving = batches[-1]
         for unit in leaving:
             tanh(unit)
         for s in range(len(leaving) + 1):
-            for first in range(0, N_BLOCKS, PAIR):
-                if pick(leaving, s) is not None:
-                    multiply(pick(leaving, s), first)
-                if pick(leaving, s - 1) is not None:
-                    turn(pick(leaving, s - 1), first, shared=True)
+            slot_work(leaving, s, True, nothing)

@@ -32,12 +32,13 @@ QUADRANTS, QUADRANT = 4, 32
 SCALE_ROWS = QUADRANT // 8
 LN_FLOOR = 2.0**-40
 
-GPSIMD_UNITS = 3
-BATCH_SIZES = (4, 4, 3, 3)
+GPSIMD_UNITS = 2
+BATCH_SIZES = (5, 4, 3, 3)
 ROOT = 128
-G_PHASE = (1, 2, 3)
-G_ORDER = "c0 c1 d0 c2 d1 d2"
-G_INVERT = ((0, 0), (1, 4), (2, 3))
+G_AFTER = (9, 12)
+G_FENCE = True
+G_ORDER = "c0 c1 d0 d1"
+G_INVERT_AFTER = (4, 7)
 SCALAR_BLOCKS = (1, 3)
 P1_LAG = 0
 FIRST_SPLIT = 1
@@ -342,11 +343,14 @@ def tile_gnn_layer_pb_t_kernel(
             quantise(position)
         for unit in batches[0]:
             log(unit)
+        fence = keep.tile([P, 4], U8)
+        if G_FENCE:
+            nc.gpsimd.tensor_copy(out=fence[:], in_=code_scales[:, round_order[-1], 0:4])
         g_steps = G_ORDER.split()
 
-        def gpsimd_work(phase, s):
+        def gpsimd_work(taken):
             for i, unit in enumerate(gpsimd_units):
-                if G_INVERT[i] == (phase, s):
+                if G_INVERT_AFTER[i] == taken:
                     while "c%d" % i in g_steps:
                         step = g_steps[0]
                         g_steps.remove(step)
@@ -359,7 +363,8 @@ def tile_gnn_layer_pb_t_kernel(
                 descend(gpsimd_units[int(g_steps[0][1:])])
                 g_steps.remove(g_steps[0])
 
-        gpsimd_work(0, 0)
+        taken = [0]
+        gpsimd_work(0)
 
         def pick(units, s):
             return units[s] if 0 <= s < len(units) else None
@@ -375,12 +380,22 @@ def tile_gnn_layer_pb_t_kernel(
                     turn(pick(leaving, s - 1), first, shared=shared)
                 between()
 
+        scalar_taken = [0]
+
+        def with_gpsimd_units(batch):
+            units = []
+            for unit in batch:
+                units.append(unit)
+                scalar_taken[0] = scalar_taken[0] + 1
+                units.extend([g for i, g in enumerate(gpsimd_units) if G_AFTER[i] == scalar_taken[0]])
+            return units
+
         def nothing():
             return None
 
         for b in range(1, len(batches)):
             entering = batches[b]
-            leaving = batches[b - 1] + [unit for i, unit in enumerate(gpsimd_units) if G_PHASE[i] == b]
+            leaving = with_gpsimd_units(batches[b - 1])
             upcoming = entering[1:]
             logs = list(entering)
             nc.scalar.activation(out=table_dummy[:], in_=table_dummy[:], func=ACT.Sigmoid)
@@ -398,7 +413,9 @@ def tile_gnn_layer_pb_t_kernel(
             sigmoids_from = len(batches[b - 1]) // 2 + P1_LAG
             logs_from = (len(batches[b - 1]) + len(entering)) // 2 + LOG_LAG
             for s in range(len(leaving) + 1):
-                gpsimd_work(b, s)
+                if pick(leaving, s) is not None:
+                    taken[0] = taken[0] + 1
+                    gpsimd_work(taken[0])
                 if s >= logs_from:
                     while upcoming:
                         next_sigmoid()
@@ -411,8 +428,8 @@ def tile_gnn_layer_pb_t_kernel(
             for unit in logs:
                 log(unit)
 
-        leaving = batches[-1]
-        for unit in leaving:
+        for unit in batches[-1]:
             tanh(unit)
+        leaving = with_gpsimd_units(batches[-1])
         for s in range(len(leaving) + 1):
             slot_work(leaving, s, True, nothing)

@@ -37,10 +37,18 @@ BATCH_SIZES = (5, 4, 3, 3)
 ROOT = 128
 G_AFTER = (9, 12)
 G_FENCE = True
+LATE_ROUNDS = 0
+LATE_PHASE = 2
 G_ORDER = "c0 c1 d0 d1"
 G_INVERT_AFTER = (4, 7)
 SCALAR_BLOCKS = (1, 3)
+LAST_SCALAR = ((1, 3), (1, 3), (1, 3))
+STORE_ON_SYNC = True
 P1_LAG = 0
+LOOKAHEAD = 1
+RF_PLACE = 6
+WARM_UP = 6
+SCALAR_COPIES = 1
 FIRST_SPLIT = 1
 BIAS_RF_AT = 3
 LOG_LAG = 9
@@ -50,7 +58,7 @@ PAIR = 2
 FEATURE_BUFS = 4
 GROUPED_BUFS = 2
 GATE_BUFS = FIRST_BATCH + 4
-RESULT_BUFS = 6
+RESULT_BUFS = 10
 
 FLOPS = 2 * SAMPLES * GROUPS * D_BB * D_OUT + 2 * SAMPLES * D_RF * D_OUT
 
@@ -72,7 +80,8 @@ def tile_gnn_layer_pb_t_kernel(
 
         features = {}
         gpsimd_units = list(range(UNITS - GPSIMD_UNITS, UNITS))
-        entry_order = batches[0][1:] + [RF_UNIT] + gpsimd_units
+        entry_order = batches[0][1:] + gpsimd_units
+        entry_order.insert(RF_PLACE, RF_UNIT)
         round_order = []
         rounds_needed = {}
         for unit in entry_order:
@@ -127,6 +136,12 @@ def tile_gnn_layer_pb_t_kernel(
             )
         nc.sync.dma_start(out=bias_rows[0][0:N_BLOCKS, :], in_=b_rfbb.rearrange("(r n) -> r n", n=P))
 
+        zeros = keep.tile([P, COLS], BF16)
+        nc.vector.memset(zeros[:], 0.0)
+        for i in range(WARM_UP):
+            warm = psum.tile([P, COLS], F32, name="acc", tag="second", bufs=PAIR)
+            nc.tensor.matmul(warm[:], lhsT=zeros[:, 0:P], rhs=zeros[:], start=True, stop=True)
+
         identity = keep.tile([P, P], F32)
         make_identity(nc, identity[:])
         identity_bf16 = keep.tile([P, P], BF16)
@@ -165,9 +180,12 @@ def tile_gnn_layer_pb_t_kernel(
                         nc.tensor.transpose(
                             flipped[:, i, u, :], words[:, first + i, u:WORDS:WORDS_PER_CODE_WORD], identity[:]
                         )
-                nc.vector.tensor_copy(
-                    out=grouped[:, first : first + PAIR, :, :], in_=flipped[:].rearrange("p i u s -> p i s u")
-                )
+                if position < SCALAR_COPIES and first > 0:
+                    nc.scalar.copy(out=grouped[:, first : first + PAIR, :, :], in_=flipped[:].rearrange("p i u s -> p i s u"))
+                else:
+                    nc.vector.tensor_copy(
+                        out=grouped[:, first : first + PAIR, :, :], in_=flipped[:].rearrange("p i u s -> p i s u")
+                    )
             nc.vector.quantize_mx(
                 out=codes[:, r, :].bitcast(FP8X4),
                 scales=code_scales[:, r, :],
@@ -294,9 +312,9 @@ def tile_gnn_layer_pb_t_kernel(
 
         laid = {}
 
-        def turn(unit, first, shared=False):
+        def turn(unit, first, shared=()):
             for block in range(first, first + PAIR):
-                if shared and block in SCALAR_BLOCKS:
+                if block in shared:
                     c, j = divmod(unit - 1, QUARTERS)
                     bank = laid.get((unit, block))
                     if bank is None:
@@ -312,7 +330,10 @@ def tile_gnn_layer_pb_t_kernel(
                         )
                     result = ring.tile([P, D_OUT], F32, tag="result", bufs=RESULT_BUFS)
                     nc.scalar.copy(out=result[:], in_=bank[:])
-                    nc.scalar.dma_start(out=out[c * P : (c + 1) * P, j * BLOCKS + block, :], in_=result[:])
+                    if STORE_ON_SYNC:
+                        nc.sync.dma_start(out=out[c * P : (c + 1) * P, j * BLOCKS + block, :], in_=result[:])
+                    else:
+                        nc.scalar.dma_start(out=out[c * P : (c + 1) * P, j * BLOCKS + block, :], in_=result[:])
                     continue
                 turned = psum.tile([P, D_OUT], F32, tag="turned")
                 for nb in range(N_BLOCKS):
@@ -330,22 +351,22 @@ def tile_gnn_layer_pb_t_kernel(
         gates[RF_UNIT] = ring.tile([P, N_BLOCKS, COLS], F32, name="gate", tag="gate", bufs=GATE_BUFS)
         quantised = 0
         for unit in entry_order:
-            for position in range(quantised, rounds_needed[unit] + 1):
+            for position in range(quantised, min(rounds_needed[unit] + LOOKAHEAD, ROUNDS)):
                 quantise(position)
                 if position == 0:
                     turn_bias(1)
                 if position == BIAS_RF_AT:
                     turn_bias(0)
-            quantised = rounds_needed[unit] + 1
+            quantised = max(quantised, min(rounds_needed[unit] + LOOKAHEAD, ROUNDS))
             first_product(unit)
             sigmoid(unit)
-        for position in range(quantised, ROUNDS):
+        for position in range(quantised, ROUNDS - LATE_ROUNDS):
             quantise(position)
         for unit in batches[0]:
             log(unit)
         fence = keep.tile([P, 4], U8)
         if G_FENCE:
-            nc.gpsimd.tensor_copy(out=fence[:], in_=code_scales[:, round_order[-1], 0:4])
+            nc.gpsimd.tensor_copy(out=fence[:], in_=code_scales[:, round_order[ROUNDS - LATE_ROUNDS - 1], 0:4])
         g_steps = G_ORDER.split()
 
         def gpsimd_work(taken):
@@ -370,8 +391,8 @@ def tile_gnn_layer_pb_t_kernel(
             return units[s] if 0 <= s < len(units) else None
 
         def slot_work(leaving, s, shared, between):
-            if shared and pick(leaving, s - 1) is not None:
-                for block in SCALAR_BLOCKS:
+            if pick(leaving, s - 1) is not None:
+                for block in shared:
                     laid[(pick(leaving, s - 1), block)] = lay_rf((pick(leaving, s - 1) - 1) // QUARTERS)
             for first in range(0, N_BLOCKS, PAIR):
                 if pick(leaving, s) is not None:
@@ -422,9 +443,12 @@ def tile_gnn_layer_pb_t_kernel(
                     if logs:
                         log(logs[0])
                         logs.remove(logs[0])
-                slot_work(leaving, s, s >= logs_from, next_sigmoid if s >= sigmoids_from else nothing)
+                slot_work(leaving, s, SCALAR_BLOCKS if s >= logs_from else (), next_sigmoid if s >= sigmoids_from else nothing)
             while upcoming:
                 next_sigmoid()
+            if b == LATE_PHASE:
+                for position in range(ROUNDS - LATE_ROUNDS, ROUNDS):
+                    quantise(position)
             for unit in logs:
                 log(unit)
 
@@ -432,4 +456,4 @@ def tile_gnn_layer_pb_t_kernel(
             tanh(unit)
         leaving = with_gpsimd_units(batches[-1])
         for s in range(len(leaving) + 1):
-            slot_work(leaving, s, True, nothing)
+            slot_work(leaving, s, LAST_SCALAR[s - 1] if s >= 1 else (), nothing)

@@ -32,33 +32,25 @@ QUADRANTS, QUADRANT = 4, 32
 SCALE_ROWS = QUADRANT // 8
 LN_FLOOR = 2.0**-40
 
-GPSIMD_UNITS = 2
-BATCH_SIZES = (5, 4, 3, 3)
-ROOT = 128
-G_AFTER = (9, 12)
-G_FENCE = True
-LATE_ROUNDS = 0
-LATE_PHASE = 2
-G_ORDER = "c0 c1 d0 d1"
-G_INVERT_AFTER = (4, 7)
+GPSIMD_UNITS = 3
+BATCH_SIZES = (7, 4, 3)
+ROOT = 32
+GPSIMD_STARTS = 8
+INVERT_ROUND = 15
+INVERT_STEPS = (16, 38)
+GPSIMD_LEAVES = (7, 9, 11)
+LAG_FROM = 9
 SCALAR_BLOCKS = (1, 3)
-LAST_SCALAR = ((1, 3), (1, 3), (1, 3))
-STORE_ON_SYNC = True
-P1_LAG = 0
 LOOKAHEAD = 1
-RF_PLACE = 6
 WARM_UP = 6
-SCALAR_COPIES = 1
-FIRST_SPLIT = 1
 BIAS_RF_AT = 3
-LOG_LAG = 9
-FIRST_BATCH = BATCH_SIZES[0]
 FIRST_BANKS = N_BLOCKS
 PAIR = 2
 FEATURE_BUFS = 4
 GROUPED_BUFS = 2
-GATE_BUFS = FIRST_BATCH + 4
-RESULT_BUFS = 10
+GATE_BUFS = BATCH_SIZES[0] + 2
+NODE_BUFS = 2
+RESULT_BUFS = 9
 
 FLOPS = 2 * SAMPLES * GROUPS * D_BB * D_OUT + 2 * SAMPLES * D_RF * D_OUT
 
@@ -71,6 +63,7 @@ def tile_gnn_layer_pb_t_kernel(
     for size in BATCH_SIZES:
         start = sum(len(batch) for batch in batches)
         batches.append(list(range(start, start + size)))
+    gpsimd_units = list(range(UNITS - GPSIMD_UNITS, UNITS))
 
     with ExitStack() as stack:
         keep = stack.enter_context(tc.tile_pool(name="keep", bufs=1))
@@ -79,9 +72,7 @@ def tile_gnn_layer_pb_t_kernel(
         stack.enter_context(tc.manual_schedule())
 
         features = {}
-        gpsimd_units = list(range(UNITS - GPSIMD_UNITS, UNITS))
-        entry_order = batches[0][1:] + gpsimd_units
-        entry_order.insert(RF_PLACE, RF_UNIT)
+        entry_order = gpsimd_units[:1] + batches[0][1:] + [RF_UNIT]
         round_order = []
         rounds_needed = {}
         for unit in entry_order:
@@ -99,29 +90,26 @@ def tile_gnn_layer_pb_t_kernel(
                 c, j = divmod(r - RF_PASSES, QUARTERS)
                 piece = BB_feature[c * P : (c + 1) * P, j * BLOCKS : (j + 1) * BLOCKS, :]
             features[r] = ring.tile([P, BLOCKS, K_PASS], BF16, name="features", tag="features", bufs=FEATURE_BUFS)
-            if position == 0 and FIRST_SPLIT > 1:
-                step = BLOCKS // FIRST_SPLIT
-                for i in range(0, BLOCKS, step):
-                    nc.sync.dma_start(out=features[r][:, i : i + step, :], in_=piece[:, i : i + step, :])
-            else:
-                nc.sync.dma_start(out=features[r][:], in_=piece)
+            nc.sync.dma_start(out=features[r][:], in_=piece)
 
         load_features(0)
         load_features(1)
 
         w_words = keep.tile([P, W_PASSES, 2 * D_OUT], U8, align_bytes=64)
         w_scales = keep.tile([P, W_PASSES, D_OUT], U8, align_bytes=64)
-        nc.vector.memset(w_scales[:].bitcast(I32), 0)
         bias_rows = {}
-        for kind in range(2):
+        for kind in (1, 0):
             bias_rows[kind] = keep.tile([P, P], BF16, name="bias_rows%d" % kind)
+            if kind == 0:
+                nc.vector.memset(w_scales[:].bitcast(I32), 0)
             nc.vector.memset(bias_rows[kind][:], 0.0)
+            if kind == 1:
+                nc.scalar.dma_start(out=bias_rows[1][0:N_BLOCKS, :], in_=b_bbbb.rearrange("(r n) -> r n", n=P))
         for quadrant in range(QUADRANTS):
             live = slice(QUADRANT * quadrant, QUADRANT * quadrant + SCALE_ROWS)
             rows = slice(SCALE_ROWS * quadrant, SCALE_ROWS * (quadrant + 1))
             nc.sync.dma_start(out=w_scales[live, RF_PASSES, :].bitcast(I32), in_=W_bbbb_scales.bitcast(I32)[0, rows, :])
         nc.sync.dma_start(out=w_words[:, RF_PASSES, :].bitcast(I32), in_=W_bbbb_words.bitcast(I32)[0])
-        nc.scalar.dma_start(out=bias_rows[1][0:N_BLOCKS, :], in_=b_bbbb.rearrange("(r n) -> r n", n=P))
         for position in range(2, FEATURE_BUFS):
             load_features(position)
         nc.sync.dma_start(
@@ -167,31 +155,45 @@ def tile_gnn_layer_pb_t_kernel(
         codes = keep.tile([P, ROUNDS, COLS], U32, align_bytes=64)
         code_scales = keep.tile([P, ROUNDS, COLS], U8, align_bytes=64)
 
-        def quantise(position):
+        grouped_tiles = {}
+
+        def bring(position, first):
             r = round_order[position]
             words = features[r][:].bitcast(F32)
-            grouped = ring.tile(
-                [P, BLOCKS, P, WORDS_PER_CODE_WORD], F32, name="grouped", tag="grouped", bufs=GROUPED_BUFS, align_bytes=64
+            if first == 0:
+                grouped_tiles[position] = ring.tile(
+                    [P, BLOCKS, P, WORDS_PER_CODE_WORD], F32, name="grouped", tag="grouped", bufs=GROUPED_BUFS, align_bytes=64
+                )
+            grouped = grouped_tiles[position]
+            flipped = psum.tile(
+                [P, PAIR, WORDS_PER_CODE_WORD, P], F32, name="flipped", tag="turned" if first == 0 else "second", bufs=PAIR
             )
-            for first in range(0, BLOCKS, PAIR):
-                flipped = psum.tile([P, PAIR, WORDS_PER_CODE_WORD, P], F32, tag="turned")
-                for i in range(PAIR):
-                    for u in range(WORDS_PER_CODE_WORD):
-                        nc.tensor.transpose(
-                            flipped[:, i, u, :], words[:, first + i, u:WORDS:WORDS_PER_CODE_WORD], identity[:]
-                        )
-                if position < SCALAR_COPIES and first > 0:
-                    nc.scalar.copy(out=grouped[:, first : first + PAIR, :, :], in_=flipped[:].rearrange("p i u s -> p i s u"))
-                else:
-                    nc.vector.tensor_copy(
-                        out=grouped[:, first : first + PAIR, :, :], in_=flipped[:].rearrange("p i u s -> p i s u")
-                    )
+            for i in range(PAIR):
+                for u in range(WORDS_PER_CODE_WORD):
+                    nc.tensor.transpose(flipped[:, i, u, :], words[:, first + i, u:WORDS:WORDS_PER_CODE_WORD], identity[:])
+            copy = nc.scalar.copy if position == 0 and first > 0 else nc.vector.tensor_copy
+            copy(out=grouped[:, first : first + PAIR, :, :], in_=flipped[:].rearrange("p i u s -> p i s u"))
+
+        def pack(position):
+            r = round_order[position]
             nc.vector.quantize_mx(
                 out=codes[:, r, :].bitcast(FP8X4),
                 scales=code_scales[:, r, :],
-                in_=grouped[:].rearrange("p i s u -> p (i s u)").bitcast(BF16),
+                in_=grouped_tiles[position][:].rearrange("p i s u -> p (i s u)").bitcast(BF16),
             )
             load_features(position + FEATURE_BUFS)
+
+        def quantise(position):
+            bring(position, 0)
+            if position > LAG_FROM:
+                pack(position - 1)
+            bring(position, PAIR)
+            if position == 0:
+                turn_bias(1)
+            if position == BIAS_RF_AT:
+                turn_bias(0)
+            if position < LAG_FROM or position == ROUNDS - 1:
+                pack(position)
 
         def product(unit, nb, tag, banks):
             if unit == RF_UNIT:
@@ -211,26 +213,21 @@ def tile_gnn_layer_pb_t_kernel(
                 )
             return acc
 
-        rf_mish = keep.tile([P, N_BLOCKS, COLS], F32)
-        gates = {}
+        rf_gate = keep.tile([P, N_BLOCKS, COLS], F32)
+        gates = {RF_UNIT: rf_gate}
         mished = {}
 
-        firsts = {}
-
-        def first_product(unit):
-            firsts[unit] = [product(unit, nb, "first", FIRST_BANKS) for nb in range(N_BLOCKS)]
-
-        def sigmoid(unit):
-            if unit in gpsimd_units:
-                gates[unit] = ring.tile([P, N_BLOCKS, COLS], F32, name="gate_g", tag="gate_g", bufs=GPSIMD_UNITS)
+        def enter(unit, first):
             if unit not in gates:
-                gates[unit] = ring.tile([P, N_BLOCKS, COLS], F32, name="gate", tag="gate", bufs=GATE_BUFS)
-            for nb in range(N_BLOCKS):
+                kind, bufs = ("gate_g", GPSIMD_UNITS) if unit in gpsimd_units else ("gate", GATE_BUFS)
+                gates[unit] = ring.tile([P, N_BLOCKS, COLS], F32, name=kind, tag=kind, bufs=bufs)
+            accs = [product(unit, nb, "first", FIRST_BANKS) for nb in range(first, first + PAIR)]
+            for i, acc in enumerate(accs):
                 nc.scalar.activation(
-                    out=gates[unit][:, nb, :],
-                    in_=firsts[unit][nb][:],
+                    out=gates[unit][:, first + i, :],
+                    in_=acc[:],
                     func=ACT.Sigmoid,
-                    bias=bias_column(minus_bias, unit, nb),
+                    bias=bias_column(minus_bias, unit, first + i),
                     scale=-1.0,
                 )
 
@@ -255,7 +252,7 @@ def tile_gnn_layer_pb_t_kernel(
             products[unit] = [leaves]
             width = N_BLOCKS * COLS // 2
             while width >= ROOT:
-                node = ring.tile([P, width], F32, name="node%d" % width, tag="node%d" % width, bufs=PAIR)
+                node = ring.tile([P, width], F32, name="node%d" % width, tag="node%d" % width, bufs=NODE_BUFS)
                 below = products[unit][-1]
                 nc.gpsimd.tensor_tensor(out=node[:], in0=below[:, 0:width], in1=below[:, width : 2 * width], op=ALU.mult)
                 products[unit].append(node[:])
@@ -283,7 +280,7 @@ def tile_gnn_layer_pb_t_kernel(
 
         def multiply(unit, first):
             if first == 0:
-                mished[unit] = rf_mish if unit == RF_UNIT else gates[unit]
+                mished[unit] = gates[unit]
             for nb in range(first, first + PAIR):
                 acc = product(unit, nb, "second", PAIR)
                 nc.vector.scalar_tensor_tensor(
@@ -302,7 +299,7 @@ def tile_gnn_layer_pb_t_kernel(
             for nb in range(N_BLOCKS):
                 nc.tensor.matmul(
                     bank[:, nb * P : (nb + 1) * P],
-                    lhsT=rf_mish[:, nb, c * P : (c + 1) * P],
+                    lhsT=rf_gate[:, nb, c * P : (c + 1) * P],
                     rhs=identity[:],
                     is_transpose=True,
                     start=(nb == 0),
@@ -310,15 +307,13 @@ def tile_gnn_layer_pb_t_kernel(
                 )
             return bank
 
-        laid = {}
-
-        def turn(unit, first, shared=()):
+        def turn(unit, first, shared):
             for block in range(first, first + PAIR):
-                if block in shared:
+                if unit != RF_UNIT:
                     c, j = divmod(unit - 1, QUARTERS)
-                    bank = laid.get((unit, block))
-                    if bank is None:
-                        bank = lay_rf(c)
+                    result = ring.tile([P, D_OUT], F32, name="result", tag="result", bufs=RESULT_BUFS)
+                if block in shared:
+                    bank = lay_rf(c)
                     for nb in range(N_BLOCKS):
                         nc.tensor.matmul(
                             bank[:, nb * P : (nb + 1) * P],
@@ -328,132 +323,95 @@ def tile_gnn_layer_pb_t_kernel(
                             start=False,
                             stop=(nb == N_BLOCKS - 1),
                         )
-                    result = ring.tile([P, D_OUT], F32, tag="result", bufs=RESULT_BUFS)
                     nc.scalar.copy(out=result[:], in_=bank[:])
-                    if STORE_ON_SYNC:
-                        nc.sync.dma_start(out=out[c * P : (c + 1) * P, j * BLOCKS + block, :], in_=result[:])
-                    else:
-                        nc.scalar.dma_start(out=out[c * P : (c + 1) * P, j * BLOCKS + block, :], in_=result[:])
-                    continue
-                turned = psum.tile([P, D_OUT], F32, tag="turned")
-                for nb in range(N_BLOCKS):
-                    nc.tensor.transpose(
-                        turned[:, nb * P : (nb + 1) * P], mished[unit][:, slot(unit, nb), block * P : (block + 1) * P], identity[:]
-                    )
-                if unit == RF_UNIT:
-                    nc.vector.tensor_copy(out=rf_term[:, block, :], in_=turned[:])
                 else:
-                    c, j = divmod(unit - 1, QUARTERS)
-                    result = ring.tile([P, D_OUT], F32, tag="result", bufs=RESULT_BUFS)
-                    nc.vector.tensor_tensor(out=result[:], in0=turned[:], in1=rf_term[:, c, :], op=ALU.add)
+                    turned = psum.tile([P, D_OUT], F32, name="turned", tag="turned", bufs=PAIR)
+                    for nb in range(N_BLOCKS):
+                        nc.tensor.transpose(
+                            turned[:, nb * P : (nb + 1) * P], mished[unit][:, slot(unit, nb), block * P : (block + 1) * P], identity[:]
+                        )
+                    if unit == RF_UNIT:
+                        nc.vector.tensor_copy(out=rf_term[:, block, :], in_=turned[:])
+                    else:
+                        nc.vector.tensor_tensor(out=result[:], in0=turned[:], in1=rf_term[:, c, :], op=ALU.add)
+                if unit != RF_UNIT:
                     nc.sync.dma_start(out=out[c * P : (c + 1) * P, j * BLOCKS + block, :], in_=result[:])
 
-        gates[RF_UNIT] = ring.tile([P, N_BLOCKS, COLS], F32, name="gate", tag="gate", bufs=GATE_BUFS)
         quantised = 0
-        for unit in entry_order:
-            for position in range(quantised, min(rounds_needed[unit] + LOOKAHEAD, ROUNDS)):
+        fence = keep.tile([P, 4], U8)
+
+        def quantise_to(end):
+            for position in range(quantised, end):
                 quantise(position)
-                if position == 0:
-                    turn_bias(1)
-                if position == BIAS_RF_AT:
-                    turn_bias(0)
-            quantised = max(quantised, min(rounds_needed[unit] + LOOKAHEAD, ROUNDS))
-            first_product(unit)
-            sigmoid(unit)
-        for position in range(quantised, ROUNDS - LATE_ROUNDS):
-            quantise(position)
+                if position == GPSIMD_STARTS:
+                    nc.gpsimd.tensor_copy(out=fence[:], in_=code_scales[:, round_order[position], 0:4])
+                    climb(gpsimd_units[0])
+                if position == INVERT_ROUND:
+                    invert(gpsimd_units[0])
+                    descend(gpsimd_units[0])
+            return max(quantised, end)
+
+        for unit in entry_order:
+            quantised = quantise_to(min(rounds_needed[unit] + LOOKAHEAD, ROUNDS))
+            for first in range(0, N_BLOCKS, PAIR):
+                enter(unit, first)
+        quantised = quantise_to(ROUNDS)
         for unit in batches[0]:
             log(unit)
-        fence = keep.tile([P, 4], U8)
-        if G_FENCE:
-            nc.gpsimd.tensor_copy(out=fence[:], in_=code_scales[:, round_order[ROUNDS - LATE_ROUNDS - 1], 0:4])
-        g_steps = G_ORDER.split()
 
-        def gpsimd_work(taken):
-            for i, unit in enumerate(gpsimd_units):
-                if G_INVERT_AFTER[i] == taken:
-                    while "c%d" % i in g_steps:
-                        step = g_steps[0]
-                        g_steps.remove(step)
-                        if step[0] == "c":
-                            climb(gpsimd_units[int(step[1:])])
-                        else:
-                            descend(gpsimd_units[int(step[1:])])
-                    invert(unit)
-            while g_steps and g_steps[0][0] == "d" and gpsimd_units[int(g_steps[0][1:])] in roots:
-                descend(gpsimd_units[int(g_steps[0][1:])])
-                g_steps.remove(g_steps[0])
-
+        steps_done = [0]
         taken = [0]
-        gpsimd_work(0)
 
-        def pick(units, s):
-            return units[s] if 0 <= s < len(units) else None
-
-        def slot_work(leaving, s, shared, between):
-            if pick(leaving, s - 1) is not None:
-                for block in shared:
-                    laid[(pick(leaving, s - 1), block)] = lay_rf((pick(leaving, s - 1) - 1) // QUARTERS)
-            for first in range(0, N_BLOCKS, PAIR):
-                if pick(leaving, s) is not None:
-                    multiply(pick(leaving, s), first)
-                if pick(leaving, s - 1) is not None:
-                    turn(pick(leaving, s - 1), first, shared=shared)
-                between()
-
-        scalar_taken = [0]
-
-        def with_gpsimd_units(batch):
+        def vector_steps(batch):
             units = []
             for unit in batch:
                 units.append(unit)
-                scalar_taken[0] = scalar_taken[0] + 1
-                units.extend([g for i, g in enumerate(gpsimd_units) if G_AFTER[i] == scalar_taken[0]])
-            return units
+                taken[0] = taken[0] + 1
+                units.extend([g for i, g in enumerate(gpsimd_units) if GPSIMD_LEAVES[i] == taken[0]])
+            steps = []
+            for s in range(len(units) + 1):
+                for first in range(0, N_BLOCKS, PAIR):
+                    if s < len(units):
+                        steps.append((multiply, units[s], first))
+                    if s > 0:
+                        steps.append((turn, units[s - 1], first))
+            return steps
 
-        def nothing():
-            return None
+        def make_step(step, shared):
+            what, unit, first = step
+            steps_done[0] = steps_done[0] + 1
+            for i, g in enumerate(gpsimd_units[1:]):
+                if INVERT_STEPS[i] == steps_done[0]:
+                    climb(g)
+                    invert(g)
+                    descend(g)
+            if what == multiply:
+                multiply(unit, first)
+            else:
+                turn(unit, first, shared)
 
         for b in range(1, len(batches)):
-            entering = batches[b]
-            leaving = with_gpsimd_units(batches[b - 1])
-            upcoming = entering[1:]
-            logs = list(entering)
             nc.scalar.activation(out=table_dummy[:], in_=table_dummy[:], func=ACT.Sigmoid)
+            waiting = [(unit, first) for unit in batches[b] for first in range(0, N_BLOCKS, PAIR)]
+            if b == 1:
+                for first in range(0, N_BLOCKS, PAIR):
+                    enter(gpsimd_units[1], first)
+                waiting = [(gpsimd_units[2], first) for first in range(0, N_BLOCKS, PAIR)] + waiting
             for unit in batches[b - 1]:
                 tanh(unit)
-            first_product(entering[0])
-            sigmoid(entering[0])
-
-            def next_sigmoid():
-                if upcoming:
-                    first_product(upcoming[0])
-                    sigmoid(upcoming[0])
-                    upcoming.remove(upcoming[0])
-
-            sigmoids_from = len(batches[b - 1]) // 2 + P1_LAG
-            logs_from = (len(batches[b - 1]) + len(entering)) // 2 + LOG_LAG
-            for s in range(len(leaving) + 1):
-                if pick(leaving, s) is not None:
-                    taken[0] = taken[0] + 1
-                    gpsimd_work(taken[0])
-                if s >= logs_from:
-                    while upcoming:
-                        next_sigmoid()
-                    if logs:
-                        log(logs[0])
-                        logs.remove(logs[0])
-                slot_work(leaving, s, SCALAR_BLOCKS if s >= logs_from else (), next_sigmoid if s >= sigmoids_from else nothing)
-            while upcoming:
-                next_sigmoid()
-            if b == LATE_PHASE:
-                for position in range(ROUNDS - LATE_ROUNDS, ROUNDS):
-                    quantise(position)
-            for unit in logs:
-                log(unit)
+            for unit, first in waiting[:PAIR]:
+                enter(unit, first)
+            waiting = waiting[PAIR:]
+            for s, step in enumerate(vector_steps(batches[b - 1])):
+                make_step(step, ())
+                if s >= 2 * len(batches[b - 1]) and waiting:
+                    enter(waiting[0][0], waiting[0][1])
+                    waiting.remove(waiting[0])
+                    if not waiting:
+                        for unit in batches[b]:
+                            log(unit)
 
         for unit in batches[-1]:
             tanh(unit)
-        leaving = with_gpsimd_units(batches[-1])
-        for s in range(len(leaving) + 1):
-            slot_work(leaving, s, LAST_SCALAR[s - 1] if s >= 1 else (), nothing)
+        for step in vector_steps(batches[-1]):
+            make_step(step, SCALAR_BLOCKS)

@@ -37,11 +37,16 @@ BATCH_SIZES = (7, 4, 3)
 ROOT = 32
 GPSIMD_STARTS = 8
 INVERT_ROUND = 15
-INVERT_STEPS = (16, 38)
-GPSIMD_LEAVES = (7, 9, 11)
+INVERT_STEPS = (22, 45)
+GPSIMD_LEAVES = (7, 10, 14)
 LAG_FROM = 9
-SCALAR_BLOCKS = (1, 3)
+SCALAR_BLOCKS = (0, 2)
 LOOKAHEAD = 1
+LA_FROM = 3
+PRELAY = 2
+TANH_FIRST = 2
+PRE_STEP = (8, 0)
+FPS = (13, 7)
 WARM_UP = 6
 BIAS_RF_AT = 3
 FIRST_BANKS = N_BLOCKS
@@ -307,13 +312,15 @@ def tile_gnn_layer_pb_t_kernel(
                 )
             return bank
 
+        laid = {}
+
         def turn(unit, first, shared):
             for block in range(first, first + PAIR):
                 if unit != RF_UNIT:
                     c, j = divmod(unit - 1, QUARTERS)
                     result = ring.tile([P, D_OUT], F32, name="result", tag="result", bufs=RESULT_BUFS)
                 if block in shared:
-                    bank = lay_rf(c)
+                    bank = laid[(unit, block)] if (unit, block) in laid else lay_rf(c)
                     for nb in range(N_BLOCKS):
                         nc.tensor.matmul(
                             bank[:, nb * P : (nb + 1) * P],
@@ -351,8 +358,8 @@ def tile_gnn_layer_pb_t_kernel(
                     descend(gpsimd_units[0])
             return max(quantised, end)
 
-        for unit in entry_order:
-            quantised = quantise_to(min(rounds_needed[unit] + LOOKAHEAD, ROUNDS))
+        for i, unit in enumerate(entry_order):
+            quantised = quantise_to(min(rounds_needed[unit] + (LOOKAHEAD if i < LA_FROM else 2), ROUNDS))
             for first in range(0, N_BLOCKS, PAIR):
                 enter(unit, first)
         quantised = quantise_to(ROUNDS)
@@ -394,22 +401,28 @@ def tile_gnn_layer_pb_t_kernel(
             nc.scalar.activation(out=table_dummy[:], in_=table_dummy[:], func=ACT.Sigmoid)
             waiting = [(unit, first) for unit in batches[b] for first in range(0, N_BLOCKS, PAIR)]
             if b == 1:
-                for first in range(0, N_BLOCKS, PAIR):
-                    enter(gpsimd_units[1], first)
                 waiting = [(gpsimd_units[2], first) for first in range(0, N_BLOCKS, PAIR)] + waiting
-            for unit in batches[b - 1]:
+            for i, unit in enumerate(batches[b - 1]):
+                if b == 1 and i == TANH_FIRST:
+                    for first in range(0, N_BLOCKS, PAIR):
+                        enter(gpsimd_units[1], first)
                 tanh(unit)
-            for unit, first in waiting[:PAIR]:
-                enter(unit, first)
-            waiting = waiting[PAIR:]
             for s, step in enumerate(vector_steps(batches[b - 1])):
+                if s == PRE_STEP[b - 1]:
+                    for unit, first in waiting[:PAIR]:
+                        enter(unit, first)
+                    waiting = waiting[PAIR:]
                 make_step(step, ())
-                if s >= 2 * len(batches[b - 1]) and waiting:
+                if s >= FPS[b - 1] and waiting:
                     enter(waiting[0][0], waiting[0][1])
                     waiting.remove(waiting[0])
                     if not waiting:
                         for unit in batches[b]:
                             log(unit)
+                        if b == len(batches) - 1:
+                            for i in range(PRELAY):
+                                unit, block = batches[-1][i // len(SCALAR_BLOCKS)], SCALAR_BLOCKS[i % len(SCALAR_BLOCKS)]
+                                laid[(unit, block)] = lay_rf((unit - 1) // QUARTERS)
 
         for unit in batches[-1]:
             tanh(unit)

@@ -35,6 +35,7 @@ LN_FLOOR = 2.0**-40
 GPSIMD_UNITS = 3
 BATCH_SIZES = (7, 4, 3)
 ROOT = 32
+SHORT = 512
 GPSIMD_STARTS = 8
 INVERT_ROUND = 15
 INVERT_STEPS = (22, 45)
@@ -47,7 +48,7 @@ PRELAY = 2
 TANH_FIRST = 2
 PRE_STEP = (8, 0)
 FPS = (13, 7)
-WARM_UP = 6
+WARM_UP = 4
 BIAS_RF_AT = 3
 FIRST_BANKS = N_BLOCKS
 PAIR = 2
@@ -95,10 +96,12 @@ def tile_gnn_layer_pb_t_kernel(
                 c, j = divmod(r - RF_PASSES, QUARTERS)
                 piece = BB_feature[c * P : (c + 1) * P, j * BLOCKS : (j + 1) * BLOCKS, :]
             features[r] = ring.tile([P, BLOCKS, K_PASS], BF16, name="features", tag="features", bufs=FEATURE_BUFS)
-            nc.sync.dma_start(out=features[r][:], in_=piece)
+            halves = PAIR if position == 0 else 1
+            step = BLOCKS // halves
+            for i in range(0, BLOCKS, step):
+                nc.sync.dma_start(out=features[r][:, i : i + step, :], in_=piece[:, i : i + step, :])
 
         load_features(0)
-        load_features(1)
 
         w_words = keep.tile([P, W_PASSES, 2 * D_OUT], U8, align_bytes=64)
         w_scales = keep.tile([P, W_PASSES, D_OUT], U8, align_bytes=64)
@@ -109,13 +112,13 @@ def tile_gnn_layer_pb_t_kernel(
                 nc.vector.memset(w_scales[:].bitcast(I32), 0)
             nc.vector.memset(bias_rows[kind][:], 0.0)
             if kind == 1:
-                nc.scalar.dma_start(out=bias_rows[1][0:N_BLOCKS, :], in_=b_bbbb.rearrange("(r n) -> r n", n=P))
+                nc.gpsimd.dma_start(out=bias_rows[1][0:N_BLOCKS, :], in_=b_bbbb.rearrange("(r n) -> r n", n=P))
         for quadrant in range(QUADRANTS):
             live = slice(QUADRANT * quadrant, QUADRANT * quadrant + SCALE_ROWS)
             rows = slice(SCALE_ROWS * quadrant, SCALE_ROWS * (quadrant + 1))
             nc.sync.dma_start(out=w_scales[live, RF_PASSES, :].bitcast(I32), in_=W_bbbb_scales.bitcast(I32)[0, rows, :])
         nc.sync.dma_start(out=w_words[:, RF_PASSES, :].bitcast(I32), in_=W_bbbb_words.bitcast(I32)[0])
-        for position in range(2, FEATURE_BUFS):
+        for position in range(1, FEATURE_BUFS):
             load_features(position)
         nc.sync.dma_start(
             out=w_words[:, 0:RF_PASSES, :].bitcast(I32), in_=W_rfbb_words.bitcast(I32).rearrange("g p w -> p g w")
@@ -250,16 +253,28 @@ def tile_gnn_layer_pb_t_kernel(
         products = {}
         roots = {}
 
+        def pool_product(out, in0, in1, width, piece):
+            for low in range(0, width, piece):
+                part = slice(low, min(low + piece, width))
+                nc.gpsimd.tensor_tensor(out=out[:, part], in0=in0[:, part], in1=in1[:, part], op=ALU.mult)
+
+        def pool_affine(part, width, scale, shift, piece):
+            for low in range(0, width, piece):
+                some = part[:, low : min(low + piece, width)]
+                nc.gpsimd.tensor_scalar(out=some, in0=some, scalar1=scale, scalar2=shift, op0=ALU.mult, op1=ALU.add)
+
         def climb(unit):
+            piece = SHORT if unit == gpsimd_units[0] else N_BLOCKS * COLS
             leaves = gates[unit][:].rearrange("p a c -> p (a c)")
-            nc.gpsimd.tensor_tensor(out=leaves, in0=leaves, in1=leaves, op=ALU.mult)
-            nc.gpsimd.tensor_scalar(out=leaves, in0=leaves, scalar1=1.0, scalar2=1.0, op0=ALU.mult, op1=ALU.add)
+            width = N_BLOCKS * COLS
+            pool_product(leaves, leaves, leaves, width, piece)
+            pool_affine(leaves, width, 1.0, 1.0, 2 * piece)
             products[unit] = [leaves]
-            width = N_BLOCKS * COLS // 2
+            width = width // 2
             while width >= ROOT:
                 node = ring.tile([P, width], F32, name="node%d" % width, tag="node%d" % width, bufs=NODE_BUFS)
                 below = products[unit][-1]
-                nc.gpsimd.tensor_tensor(out=node[:], in0=below[:, 0:width], in1=below[:, width : 2 * width], op=ALU.mult)
+                pool_product(node[:], below[:, 0:width], below[:, width : 2 * width], width, piece)
                 products[unit].append(node[:])
                 width = width // 2
 
@@ -269,19 +284,20 @@ def tile_gnn_layer_pb_t_kernel(
             roots[unit] = root[:]
 
         def descend(unit):
+            piece = SHORT if unit == gpsimd_units[0] else N_BLOCKS * COLS
             inverse = roots[unit]
             width = ROOT
             for level in reversed(products[unit][1:-1]):
                 lower = ring.tile([P, 2 * width], F32, name="lower%d" % width, tag="lower%d" % width, bufs=1)
-                nc.gpsimd.tensor_tensor(out=lower[:, 0:width], in0=level[:, width : 2 * width], in1=inverse, op=ALU.mult)
-                nc.gpsimd.tensor_tensor(out=lower[:, width : 2 * width], in0=level[:, 0:width], in1=inverse, op=ALU.mult)
+                pool_product(lower[:, 0:width], level[:, width : 2 * width], inverse, width, piece)
+                pool_product(lower[:, width : 2 * width], level[:, 0:width], inverse, width, piece)
                 inverse = lower[:]
                 width = 2 * width
             leaves = products[unit][0]
             for half in range(2):
                 part = leaves[:, half * width : (half + 1) * width]
-                nc.gpsimd.tensor_tensor(out=part, in0=part, in1=inverse, op=ALU.mult)
-            nc.gpsimd.tensor_scalar(out=leaves, in0=leaves, scalar1=2.0, scalar2=-1.0, op0=ALU.mult, op1=ALU.add)
+                pool_product(part, part, inverse, width, piece)
+            pool_affine(leaves, 2 * width, 2.0, -1.0, 2 * piece)
 
         def multiply(unit, first):
             if first == 0:

@@ -56,7 +56,7 @@ FEATURE_BUFS = 4
 GROUPED_BUFS = 2
 GATE_BUFS = BATCH_SIZES[0] + 2
 NODE_BUFS = 2
-RESULT_BUFS = 9
+RESULT_BUFS = 3
 
 FLOPS = 2 * SAMPLES * GROUPS * D_BB * D_OUT + 2 * SAMPLES * D_RF * D_OUT
 
@@ -329,12 +329,17 @@ def tile_gnn_layer_pb_t_kernel(
             return bank
 
         laid = {}
+        results = {}
+        last_phase = []
 
         def turn(unit, first, shared):
+            if unit != RF_UNIT:
+                c, j = divmod(unit - 1, QUARTERS)
+                place = out[c * P : (c + 1) * P, j * BLOCKS : (j + 1) * BLOCKS, :]
+                if first == 0:
+                    results[unit] = ring.tile([P, BLOCKS, D_OUT], F32, name="result", tag="result", bufs=RESULT_BUFS)
+                result = results[unit]
             for block in range(first, first + PAIR):
-                if unit != RF_UNIT:
-                    c, j = divmod(unit - 1, QUARTERS)
-                    result = ring.tile([P, D_OUT], F32, name="result", tag="result", bufs=RESULT_BUFS)
                 if block in shared:
                     bank = laid[(unit, block)] if (unit, block) in laid else lay_rf(c)
                     for nb in range(N_BLOCKS):
@@ -346,7 +351,7 @@ def tile_gnn_layer_pb_t_kernel(
                             start=False,
                             stop=(nb == N_BLOCKS - 1),
                         )
-                    nc.scalar.copy(out=result[:], in_=bank[:])
+                    nc.scalar.copy(out=result[:, block, :], in_=bank[:])
                 else:
                     turned = psum.tile([P, D_OUT], F32, name="turned", tag="turned", bufs=PAIR)
                     for nb in range(N_BLOCKS):
@@ -356,9 +361,11 @@ def tile_gnn_layer_pb_t_kernel(
                     if unit == RF_UNIT:
                         nc.vector.tensor_copy(out=rf_term[:, block, :], in_=turned[:])
                     else:
-                        nc.vector.tensor_tensor(out=result[:], in0=turned[:], in1=rf_term[:, c, :], op=ALU.add)
-                if unit != RF_UNIT:
-                    nc.sync.dma_start(out=out[c * P : (c + 1) * P, j * BLOCKS + block, :], in_=result[:])
+                        nc.vector.tensor_tensor(out=result[:, block, :], in0=turned[:], in1=rf_term[:, c, :], op=ALU.add)
+                if unit != RF_UNIT and last_phase:
+                    nc.sync.dma_start(out=place[:, block : block + 1, :], in_=result[:, block : block + 1, :])
+                elif unit != RF_UNIT and block == BLOCKS - 1:
+                    nc.sync.dma_start(out=place, in_=result[:])
 
         quantised = 0
         fence = keep.tile([P, 4], U8)
@@ -440,6 +447,7 @@ def tile_gnn_layer_pb_t_kernel(
                                 unit, block = batches[-1][i // len(SCALAR_BLOCKS)], SCALAR_BLOCKS[i % len(SCALAR_BLOCKS)]
                                 laid[(unit, block)] = lay_rf((unit - 1) // QUARTERS)
 
+        last_phase.append(True)
         for unit in batches[-1]:
             tanh(unit)
         for step in vector_steps(batches[-1]):

from contextlib import ExitStack

import concourse.mybir as mybir
from concourse.masks import make_identity

F32 = mybir.dt.float32
BF16 = mybir.dt.bfloat16
I32 = mybir.dt.int32
U32 = mybir.dt.uint32
U8 = mybir.dt.uint8
FP8X4 = mybir.dt.float8_e4m3fn_x4
FP4X4 = mybir.dt.float4_e2m1fn_x4
ACT = mybir.ActivationFunctionType
ALU = mybir.AluOpType

P = 128
K_PASS = 4 * P
WORDS = K_PASS // 2
WORDS_PER_CODE_WORD = 2
SAMPLES, GROUPS, D_BB, D_RF, D_OUT = 512, 16, 512, 1024, 512
SAMPLE_BLOCKS = SAMPLES // P
BLOCKS = 4
COLS = BLOCKS * P
N_BLOCKS = D_OUT // P
QUARTERS = GROUPS // BLOCKS
RF_UNIT = 0
RF_PASSES = D_RF // K_PASS
UNITS = 1 + SAMPLE_BLOCKS * QUARTERS
ROUNDS = RF_PASSES + SAMPLE_BLOCKS * QUARTERS
W_PASSES = RF_PASSES + 1
QUADRANTS, QUADRANT = 4, 32
SCALE_ROWS = QUADRANT // 8
LN_FLOOR = 2.0**-40

GPSIMD_UNITS = 3
BATCH_SIZES = (7, 4, 3)
ROOT = 32
SHORT = 512
GPSIMD_STARTS = 8
INVERT_ROUND = 15
INVERT_STEPS = (22, 45)
GPSIMD_LEAVES = (7, 10, 14)
LAG_FROM = 9
SCALAR_BLOCKS = (0, 2)
LOOKAHEAD = 1
LA_FROM = 3
PRELAY = 2
TANH_FIRST = 2
PRE_STEP = (8, 0)
FPS = (13, 7)
WARM_UP = 4
BIAS_RF_AT = 3
FIRST_BANKS = N_BLOCKS
PAIR = 2
FEATURE_BUFS = 4
GROUPED_BUFS = 2
GATE_BUFS = BATCH_SIZES[0] + 2
NODE_BUFS = 2
RESULT_BUFS = 3

FLOPS = 2 * SAMPLES * GROUPS * D_BB * D_OUT + 2 * SAMPLES * D_RF * D_OUT


def tile_gnn_layer_pb_t_kernel(
    tc, BB_feature, RF_feature, W_bbbb_words, W_bbbb_scales, b_bbbb, W_rfbb_words, W_rfbb_scales, b_rfbb, out
):
    nc = tc.nc
    batches = []
    for size in BATCH_SIZES:
        start = sum(len(batch) for batch in batches)
        batches.append(list(range(start, start + size)))
    gpsimd_units = list(range(UNITS - GPSIMD_UNITS, UNITS))

    with ExitStack() as stack:
        keep = stack.enter_context(tc.tile_pool(name="keep", bufs=1))
        ring = stack.enter_context(tc.tile_pool(name="ring", bufs=1))
        psum = stack.enter_context(tc.psum_pool(name="psum", bufs=PAIR))
        stack.enter_context(tc.manual_schedule())

        features = {}
        entry_order = gpsimd_units[:1] + batches[0][1:] + [RF_UNIT]
        round_order = []
        rounds_needed = {}
        for unit in entry_order:
            round_order.extend(list(range(RF_PASSES)) if unit == RF_UNIT else [RF_PASSES + unit - 1])
            rounds_needed[unit] = len(round_order)
        round_order.extend([r for r in range(ROUNDS) if r not in round_order])

        def load_features(position):
            if position >= ROUNDS:
                return
            r = round_order[position]
            if r < RF_PASSES:
                piece = RF_feature.rearrange("(c s) k -> s c k", s=P)[:, :, r * K_PASS : (r + 1) * K_PASS]
            else:
                c, j = divmod(r - RF_PASSES, QUARTERS)
                piece = BB_feature[c * P : (c + 1) * P, j * BLOCKS : (j + 1) * BLOCKS, :]
            features[r] = ring.tile([P, BLOCKS, K_PASS], BF16, name="features", tag="features", bufs=FEATURE_BUFS)
            halves = PAIR if position == 0 else 1
            step = BLOCKS // halves
            for i in range(0, BLOCKS, step):
                nc.sync.dma_start(out=features[r][:, i : i + step, :], in_=piece[:, i : i + step, :])

        load_features(0)

        w_words = keep.tile([P, W_PASSES, 2 * D_OUT], U8, align_bytes=64)
        w_scales = keep.tile([P, W_PASSES, D_OUT], U8, align_bytes=64)
        bias_rows = {}
        for kind in (1, 0):
            bias_rows[kind] = keep.tile([P, P], BF16, name="bias_rows%d" % kind)
            if kind == 0:
                nc.vector.memset(w_scales[:].bitcast(I32), 0)
            nc.vector.memset(bias_rows[kind][:], 0.0)
            if kind == 1:
                nc.gpsimd.dma_start(out=bias_rows[1][0:N_BLOCKS, :], in_=b_bbbb.rearrange("(r n) -> r n", n=P))
        for quadrant in range(QUADRANTS):
            live = slice(QUADRANT * quadrant, QUADRANT * quadrant + SCALE_ROWS)
            rows = slice(SCALE_ROWS * quadrant, SCALE_ROWS * (quadrant + 1))
            nc.sync.dma_start(out=w_scales[live, RF_PASSES, :].bitcast(I32), in_=W_bbbb_scales.bitcast(I32)[0, rows, :])
        nc.sync.dma_start(out=w_words[:, RF_PASSES, :].bitcast(I32), in_=W_bbbb_words.bitcast(I32)[0])
        for position in range(1, FEATURE_BUFS):
            load_features(position)
        nc.sync.dma_start(
            out=w_words[:, 0:RF_PASSES, :].bitcast(I32), in_=W_rfbb_words.bitcast(I32).rearrange("g p w -> p g w")
        )
        for quadrant in range(QUADRANTS):
            live = slice(QUADRANT * quadrant, QUADRANT * quadrant + SCALE_ROWS)
            rows = slice(SCALE_ROWS * quadrant, SCALE_ROWS * (quadrant + 1))
            nc.sync.dma_start(
                out=w_scales[live, 0:RF_PASSES, :].bitcast(I32),
                in_=W_rfbb_scales.bitcast(I32)[:, rows, :].rearrange("g r n -> r g n"),
            )
        nc.sync.dma_start(out=bias_rows[0][0:N_BLOCKS, :], in_=b_rfbb.rearrange("(r n) -> r n", n=P))

        zeros = keep.tile([P, COLS], BF16)
        nc.vector.memset(zeros[:], 0.0)
        for i in range(WARM_UP):
            warm = psum.tile([P, COLS], F32, name="acc", tag="second", bufs=PAIR)
            nc.tensor.matmul(warm[:], lhsT=zeros[:, 0:P], rhs=zeros[:], start=True, stop=True)

        identity = keep.tile([P, P], F32)
        make_identity(nc, identity[:])
        identity_bf16 = keep.tile([P, P], BF16)
        make_identity(nc, identity_bf16[:])
        table_dummy = keep.tile([P, 1], F32)
        nc.vector.memset(table_dummy[:], 0.0)
        ln_floor = keep.tile([P, 1], F32)
        nc.vector.memset(ln_floor[:], LN_FLOOR)
        bias = keep.tile([P, 2 * N_BLOCKS], F32)
        minus_bias = keep.tile([P, 2 * N_BLOCKS], F32)

        def turn_bias(kind):
            columns = slice(kind * N_BLOCKS, (kind + 1) * N_BLOCKS)
            bias_turned = psum.tile([P, P], BF16, tag="turned")
            nc.tensor.transpose(bias_turned[:], bias_rows[kind][:], identity_bf16[:])
            nc.vector.tensor_copy(out=bias[:, columns], in_=bias_turned[:, 0:N_BLOCKS])
            nc.vector.tensor_scalar_mul(out=minus_bias[:, columns], in0=bias_turned[:, 0:N_BLOCKS], scalar1=-1.0)

        def bias_column(table, unit, nb):
            column = nb if unit == RF_UNIT else N_BLOCKS + nb
            return table[:, column : column + 1]

        codes = keep.tile([P, ROUNDS, COLS], U32, align_bytes=64)
        code_scales = keep.tile([P, ROUNDS, COLS], U8, align_bytes=64)

        grouped_tiles = {}

        def bring(position, first):
            r = round_order[position]
            words = features[r][:].bitcast(F32)
            if first == 0:
                grouped_tiles[position] = ring.tile(
                    [P, BLOCKS, P, WORDS_PER_CODE_WORD], F32, name="grouped", tag="grouped", bufs=GROUPED_BUFS, align_bytes=64
                )
            grouped = grouped_tiles[position]
            flipped = psum.tile(
                [P, PAIR, WORDS_PER_CODE_WORD, P], F32, name="flipped", tag="turned" if first == 0 else "second", bufs=PAIR
            )
            for i in range(PAIR):
                for u in range(WORDS_PER_CODE_WORD):
                    nc.tensor.transpose(flipped[:, i, u, :], words[:, first + i, u:WORDS:WORDS_PER_CODE_WORD], identity[:])
            copy = nc.scalar.copy if position == 0 and first > 0 else nc.vector.tensor_copy
            copy(out=grouped[:, first : first + PAIR, :, :], in_=flipped[:].rearrange("p i u s -> p i s u"))

        def pack(position):
            r = round_order[position]
            nc.vector.quantize_mx(
                out=codes[:, r, :].bitcast(FP8X4),
                scales=code_scales[:, r, :],
                in_=grouped_tiles[position][:].rearrange("p i s u -> p (i s u)").bitcast(BF16),
            )
            load_features(position + FEATURE_BUFS)

        def quantise(position):
            bring(position, 0)
            if position > LAG_FROM:
                pack(position - 1)
            bring(position, PAIR)
            if position == 0:
                turn_bias(1)
            if position == BIAS_RF_AT:
                turn_bias(0)
            if position < LAG_FROM or position == ROUNDS - 1:
                pack(position)

        def product(unit, nb, tag, banks):
            if unit == RF_UNIT:
                passes = [(g, g) for g in range(RF_PASSES)]
            else:
                passes = [(RF_PASSES, RF_PASSES + unit - 1)]
            acc = psum.tile([P, COLS], F32, name="acc", tag=tag, bufs=banks)
            for g, (w, r) in enumerate(passes):
                nc.tensor.matmul_mx(
                    out=acc[:],
                    lhsT=w_words[:, w, 2 * P * nb : 2 * P * (nb + 1)].bitcast(FP4X4),
                    lhsT_scale=w_scales[:, w, P * nb : P * (nb + 1)],
                    rhs=codes[:, r, :].bitcast(FP8X4),
                    rhs_scale=code_scales[:, r, :],
                    start=(g == 0),
                    stop=(g == len(passes) - 1),
                )
            return acc

        rf_gate = keep.tile([P, N_BLOCKS, COLS], F32)
        gates = {RF_UNIT: rf_gate}
        mished = {}

        def enter(unit, first):
            if unit not in gates:
                kind, bufs = ("gate_g", GPSIMD_UNITS) if unit in gpsimd_units else ("gate", GATE_BUFS)
                gates[unit] = ring.tile([P, N_BLOCKS, COLS], F32, name=kind, tag=kind, bufs=bufs)
            accs = [product(unit, nb, "first", FIRST_BANKS) for nb in range(first, first + PAIR)]
            for i, acc in enumerate(accs):
                nc.scalar.activation(
                    out=gates[unit][:, first + i, :],
                    in_=acc[:],
                    func=ACT.Sigmoid,
                    bias=bias_column(minus_bias, unit, first + i),
                    scale=-1.0,
                )

        def log(unit):
            nc.scalar.activation(out=gates[unit][:], in_=gates[unit][:], func=ACT.Ln, bias=ln_floor[:], scale=1.0)

        def tanh(unit):
            for first in range(0, N_BLOCKS, PAIR):
                part = gates[unit][:, first : first + PAIR, :]
                nc.scalar.activation(out=part, in_=part, func=ACT.Tanh, scale=-1.0)

        def slot(unit, nb):
            return (nb + N_BLOCKS // 2) % N_BLOCKS if unit in gpsimd_units else nb

        products = {}
        roots = {}

        def pool_product(out, in0, in1, width, piece):
            for low in range(0, width, piece):
                part = slice(low, min(low + piece, width))
                nc.gpsimd.tensor_tensor(out=out[:, part], in0=in0[:, part], in1=in1[:, part], op=ALU.mult)

        def pool_affine(part, width, scale, shift, piece):
            for low in range(0, width, piece):
                some = part[:, low : min(low + piece, width)]
                nc.gpsimd.tensor_scalar(out=some, in0=some, scalar1=scale, scalar2=shift, op0=ALU.mult, op1=ALU.add)

        def climb(unit):
            piece = SHORT if unit == gpsimd_units[0] else N_BLOCKS * COLS
            leaves = gates[unit][:].rearrange("p a c -> p (a c)")
            width = N_BLOCKS * COLS
            pool_product(leaves, leaves, leaves, width, piece)
            pool_affine(leaves, width, 1.0, 1.0, 2 * piece)
            products[unit] = [leaves]
            width = width // 2
            while width >= ROOT:
                node = ring.tile([P, width], F32, name="node%d" % width, tag="node%d" % width, bufs=NODE_BUFS)
                below = products[unit][-1]
                pool_product(node[:], below[:, 0:width], below[:, width : 2 * width], width, piece)
                products[unit].append(node[:])
                width = width // 2

        def invert(unit):
            root = ring.tile([P, ROOT], F32, name="root", tag="root", bufs=PAIR)
            nc.vector.reciprocal(out=root[:], in_=products[unit][-1])
            roots[unit] = root[:]

        def descend(unit):
            piece = SHORT if unit == gpsimd_units[0] else N_BLOCKS * COLS
            inverse = roots[unit]
            width = ROOT
            for level in reversed(products[unit][1:-1]):
                lower = ring.tile([P, 2 * width], F32, name="lower%d" % width, tag="lower%d" % width, bufs=1)
                pool_product(lower[:, 0:width], level[:, width : 2 * width], inverse, width, piece)
                pool_product(lower[:, width : 2 * width], level[:, 0:width], inverse, width, piece)
                inverse = lower[:]
                width = 2 * width
            leaves = products[unit][0]
            for half in range(2):
                part = leaves[:, half * width : (half + 1) * width]
                pool_product(part, part, inverse, width, piece)
            pool_affine(leaves, 2 * width, 2.0, -1.0, 2 * piece)

        def multiply(unit, first):
            if first == 0:
                mished[unit] = gates[unit]
            for nb in range(first, first + PAIR):
                acc = product(unit, nb, "second", PAIR)
                nc.vector.scalar_tensor_tensor(
                    out=mished[unit][:, slot(unit, nb), :],
                    in0=acc[:],
                    scalar=bias_column(bias, unit, nb),
                    in1=gates[unit][:, slot(unit, nb), :],
                    op0=ALU.add,
                    op1=ALU.mult,
                )

        rf_term = keep.tile([P, SAMPLE_BLOCKS, D_OUT], F32)

        def lay_rf(c):
            bank = psum.tile([P, D_OUT], F32, name="acc", tag="first", bufs=FIRST_BANKS)
            for nb in range(N_BLOCKS):
                nc.tensor.matmul(
                    bank[:, nb * P : (nb + 1) * P],
                    lhsT=rf_gate[:, nb, c * P : (c + 1) * P],
                    rhs=identity[:],
                    is_transpose=True,
                    start=(nb == 0),
                    stop=False,
                )
            return bank

        laid = {}
        results = {}
        last_phase = []

        def turn(unit, first, shared):
            if unit != RF_UNIT:
                c, j = divmod(unit - 1, QUARTERS)
                place = out[c * P : (c + 1) * P, j * BLOCKS : (j + 1) * BLOCKS, :]
                if first == 0:
                    results[unit] = ring.tile([P, BLOCKS, D_OUT], F32, name="result", tag="result", bufs=RESULT_BUFS)
                result = results[unit]
            for block in range(first, first + PAIR):
                if block in shared:
                    bank = laid[(unit, block)] if (unit, block) in laid else lay_rf(c)
                    for nb in range(N_BLOCKS):
                        nc.tensor.matmul(
                            bank[:, nb * P : (nb + 1) * P],
                            lhsT=mished[unit][:, slot(unit, nb), block * P : (block + 1) * P],
                            rhs=identity[:],
                            is_transpose=True,
                            start=False,
                            stop=(nb == N_BLOCKS - 1),
                        )
                    nc.scalar.copy(out=result[:, block, :], in_=bank[:])
                else:
                    turned = psum.tile([P, D_OUT], F32, name="turned", tag="turned", bufs=PAIR)
                    for nb in range(N_BLOCKS):
                        nc.tensor.transpose(
                            turned[:, nb * P : (nb + 1) * P], mished[unit][:, slot(unit, nb), block * P : (block + 1) * P], identity[:]
                        )
                    if unit == RF_UNIT:
                        nc.vector.tensor_copy(out=rf_term[:, block, :], in_=turned[:])
                    else:
                        nc.vector.tensor_tensor(out=result[:, block, :], in0=turned[:], in1=rf_term[:, c, :], op=ALU.add)
                if unit != RF_UNIT and last_phase:
                    nc.sync.dma_start(out=place[:, block : block + 1, :], in_=result[:, block : block + 1, :])
                elif unit != RF_UNIT and block == BLOCKS - 1:
                    nc.sync.dma_start(out=place, in_=result[:])

        quantised = 0
        fence = keep.tile([P, 4], U8)

        def quantise_to(end):
            for position in range(quantised, end):
                quantise(position)
                if position == GPSIMD_STARTS:
                    nc.gpsimd.tensor_copy(out=fence[:], in_=code_scales[:, round_order[position], 0:4])
                    climb(gpsimd_units[0])
                if position == INVERT_ROUND:
                    invert(gpsimd_units[0])
                    descend(gpsimd_units[0])
            return max(quantised, end)

        for i, unit in enumerate(entry_order):
            quantised = quantise_to(min(rounds_needed[unit] + (LOOKAHEAD if i < LA_FROM else 2), ROUNDS))
            for first in range(0, N_BLOCKS, PAIR):
                enter(unit, first)
        quantised = quantise_to(ROUNDS)
        for unit in batches[0]:
            log(unit)

        steps_done = [0]
        taken = [0]

        def vector_steps(batch):
            units = []
            for unit in batch:
                units.append(unit)
                taken[0] = taken[0] + 1
                units.extend([g for i, g in enumerate(gpsimd_units) if GPSIMD_LEAVES[i] == taken[0]])
            steps = []
            for s in range(len(units) + 1):
                for first in range(0, N_BLOCKS, PAIR):
                    if s < len(units):
                        steps.append((multiply, units[s], first))
                    if s > 0:
                        steps.append((turn, units[s - 1], first))
            return steps

        def make_step(step, shared):
            what, unit, first = step
            steps_done[0] = steps_done[0] + 1
            for i, g in enumerate(gpsimd_units[1:]):
                if INVERT_STEPS[i] == steps_done[0]:
                    climb(g)
                    invert(g)
                    descend(g)
            if what == multiply:
                multiply(unit, first)
            else:
                turn(unit, first, shared)

        for b in range(1, len(batches)):
            nc.scalar.activation(out=table_dummy[:], in_=table_dummy[:], func=ACT.Sigmoid)
            waiting = [(unit, first) for unit in batches[b] for first in range(0, N_BLOCKS, PAIR)]
            if b == 1:
                waiting = [(gpsimd_units[2], first) for first in range(0, N_BLOCKS, PAIR)] + waiting
            for i, unit in enumerate(batches[b - 1]):
                if b == 1 and i == TANH_FIRST:
                    for first in range(0, N_BLOCKS, PAIR):
                        enter(gpsimd_units[1], first)
                tanh(unit)
            for s, step in enumerate(vector_steps(batches[b - 1])):
                if s == PRE_STEP[b - 1]:
                    for unit, first in waiting[:PAIR]:
                        enter(unit, first)
                    waiting = waiting[PAIR:]
                make_step(step, ())
                if s >= FPS[b - 1] and waiting:
                    enter(waiting[0][0], waiting[0][1])
                    waiting.remove(waiting[0])
                    if not waiting:
                        for unit in batches[b]:
                            log(unit)
                        if b == len(batches) - 1:
                            for i in range(PRELAY):
                                unit, block = batches[-1][i // len(SCALAR_BLOCKS)], SCALAR_BLOCKS[i % len(SCALAR_BLOCKS)]
                                laid[(unit, block)] = lay_rf((unit - 1) // QUARTERS)

        last_phase.append(True)
        for unit in batches[-1]:
            tanh(unit)
        for step in vector_steps(batches[-1]):
            make_step(step, SCALAR_BLOCKS)
